import numpy as np
import ml_dtypes


def mxq(x, axis, fmt="e4m3"):
    dtype, down = {"e4m3": (ml_dtypes.float8_e4m3fn, 7), "e5m2": (ml_dtypes.float8_e5m2, 14)}[fmt]
    v = np.moveaxis(np.asarray(x, np.float32).astype(ml_dtypes.bfloat16).astype(np.float64), axis, -1)
    blocks = v.reshape(v.shape[:-1] + (-1, 32))
    amax = np.abs(blocks).max(-1, keepdims=True)
    byte = np.maximum(np.where(amax > 0, np.frexp(amax)[1] - 1 + 127, 0) - down, 1)
    scale = np.exp2(byte - 127.0)
    codes = (blocks / scale).astype(np.float32).astype(dtype).astype(np.float64)
    return np.moveaxis((codes * scale).reshape(v.shape), -1, axis)


WIDE = False


def mx_kscale(k):
    if not WIDE:
        return np.ones(k)
    levels = np.array([10, -10, 5, -5, 0])
    a = np.random.permutation(np.resize(levels, k // 512 * 4)).reshape(k // 512, 4)
    idx = np.arange(k)
    return np.exp2(a[idx // 512, idx % 128 // 32])


BF16 = ml_dtypes.bfloat16


def bf(x):
    return np.asarray(x, np.float32).astype(BF16)


def f64(x):
    return np.asarray(x).astype(np.float64)


B, N, D, H = 2, 512, 8192, 512
EDGE_P = 0.01
DEG = 1.0 + EDGE_P * N


def normalize_adj(adj):
    rowsum = adj.sum(axis=1)
    d_inv_sqrt = np.where(rowsum > 0, 1.0 / np.sqrt(np.maximum(rowsum, 1e-30)), 0.0)
    return d_inv_sqrt[:, :, None] * adj.transpose(0, 2, 1) * d_inv_sqrt[:, None, :]


def setup_inputs():
    s = mx_kscale(D)
    adj = (np.random.uniform(size=(B, N, N)) < EDGE_P).astype(np.float64)
    adj = np.minimum(adj + np.eye(N)[None], 1.0)
    return {"batch_graph": bf(np.random.standard_normal((B, N, D)) * s),
            "adj": bf(adj),
            "W1": bf(np.random.standard_normal((D, H)) * np.sqrt(DEG / D) / s[:, None]),
            "b1": bf(np.random.standard_normal(H) * 0.2)}


def reference(batch_graph, adj, W1, b1):
    a = normalize_adj(f64(adj))
    z = mxq(f64(batch_graph), 2, "e4m3") @ mxq(f64(W1), 0, "e4m3")
    return np.maximum((mxq(a, 2, "e4m3") @ mxq(z, 1, "e4m3")) + f64(b1), 0.0)

@@ -1,0 +1,262 @@
+from contextlib import ExitStack
+
+import concourse.mybir as mybir
+from concourse.masks import make_identity
+
+F32 = mybir.dt.float32
+BF16 = mybir.dt.bfloat16
+U32 = mybir.dt.uint32
+U8 = mybir.dt.uint8
+FP8X4 = mybir.dt.float8_e4m3fn_x4
+ALU = mybir.AluOpType
+ACT = mybir.ActivationFunctionType
+
+B, N, D, H = 2, 512, 8192, 512
+FLOPS = 2 * B * N * D * H + 2 * B * N * N * H
+
+P = 128
+PACK = 4
+K_PASS = P * PACK
+PASSES = D // K_PASS
+TILES = N // P
+PAIR_K = 2 * K_PASS
+PAIRS = PASSES // 2
+BLOCKS = 4
+ROUND_K = BLOCKS * PAIR_K
+ROUNDS = TILES * PAIRS // BLOCKS
+SCALAR_COLS = 128
+
+
+def blocks_of_round(j):
+    batch, r = divmod(j, ROUNDS)
+    if batch == 0:
+        return [(blk, r) for blk in range(BLOCKS)]
+    rounds_per_tile = PAIRS // BLOCKS
+    return [(r // rounds_per_tile, BLOCKS * (r % rounds_per_tile) + blk) for blk in range(BLOCKS)]
+
+
+def tile_perception_pa_k_kernel(tc, batch_graph, adj, W1, b1, out):
+    nc = tc.nc
+    with ExitStack() as ctx:
+        ctx.enter_context(tc.manual_schedule())
+        keep = ctx.enter_context(tc.tile_pool(name="keep", bufs=1))
+        xraw_pool = ctx.enter_context(tc.tile_pool(name="xraw", bufs=5))
+        xgrp_pool = ctx.enter_context(tc.tile_pool(name="xgrp", bufs=3))
+        xq_pool = ctx.enter_context(tc.tile_pool(name="xq", bufs=3))
+        wraw_pool = ctx.enter_context(tc.tile_pool(name="wraw", bufs=4))
+        grp_pool = ctx.enter_context(tc.tile_pool(name="grp", bufs=3))
+        work = ctx.enter_context(tc.tile_pool(name="work", bufs=2))
+        outp = ctx.enter_context(tc.tile_pool(name="outp", bufs=3))
+        acc = ctx.enter_context(tc.psum_pool(name="acc", bufs=4))
+        tr = ctx.enter_context(tc.psum_pool(name="tr", bufs=BLOCKS))
+
+        ident = keep.tile([P, P], F32)
+        make_identity(nc, ident[:])
+        ones = keep.tile([P, P], BF16)
+        nc.vector.memset(ones[:], 1.0)
+        bias_rows = keep.tile([P, H], BF16)
+        nc.vector.memset(bias_rows[:], 0.0)
+
+        adj_rows = []
+        for b in range(B):
+            adj_b = keep.tile([P, TILES, N], BF16, name="adj_rows%d" % b)
+            nc.sync.dma_start(out=adj_b[:], in_=adj[b].rearrange("(p t) i -> p t i", t=TILES))
+            adj_rows.append(adj_b)
+        nc.sync.dma_start(out=bias_rows[0:1, :], in_=b1.unsqueeze(0))
+
+        w_view = W1.rearrange("(g u q e) c -> g q u e c", u=2, q=P, e=2)
+        x_raw_of = []
+        w_raw_of = []
+        for j in range(B * ROUNDS):
+            batch = j // ROUNDS
+            x_view = batch_graph[batch].rearrange("(p t) k -> p t k", t=TILES)
+            first_tile, first_pair = blocks_of_round(j)[0]
+            x_raw = xraw_pool.tile([P, ROUND_K], BF16)
+            if batch == 0:
+                nc.sync.dma_start(
+                    out=x_raw[:].rearrange("p (t k) -> p t k", t=TILES),
+                    in_=x_view[:, :, first_pair * PAIR_K : (first_pair + 1) * PAIR_K],
+                )
+            else:
+                nc.sync.dma_start(
+                    out=x_raw[:],
+                    in_=x_view[:, first_tile, first_pair * PAIR_K : first_pair * PAIR_K + ROUND_K],
+                )
+            x_raw_of.append(x_raw)
+            if batch == 0:
+                for g in (2 * j, 2 * j + 1):
+                    w_raw = wraw_pool.tile([P, PACK, H], BF16)
+                    nc.sync.dma_start(
+                        out=w_raw[:].rearrange("q (u e) c -> q u e c", u=2), in_=w_view[g]
+                    )
+                    w_raw_of.append(w_raw)
+
+        c_sums = []
+        c_floors = []
+        for b in range(B):
+            c_sum = acc.tile([P, N], F32, tag="acc")
+            for t in range(TILES):
+                nc.tensor.matmul(
+                    out=c_sum[:], lhsT=ones[:], rhs=adj_rows[b][:, t, :],
+                    start=(t == 0), stop=(t == TILES - 1),
+                )
+            c_by_tile = c_sum[:].rearrange("m (q t) -> m t q", t=TILES)
+            c_floor = work.tile([P, TILES, P], F32)
+            nc.vector.tensor_scalar_max(out=c_floor[:], in0=c_by_tile, scalar1=1e-30)
+            c_sums.append(c_by_tile)
+            c_floors.append(c_floor)
+        bias_sum = acc.tile([P, H], F32, tag="acc")
+        nc.tensor.matmul(out=bias_sum[:], lhsT=ones[:], rhs=bias_rows[:], start=True, stop=True)
+        roots = []
+        for b in range(B):
+            root = work.tile([P, TILES, P], F32)
+            nc.scalar.sqrt(out=root[:], in_=c_floors[b][:])
+            roots.append(root)
+        bias_all = keep.tile([P, H], F32)
+        nc.scalar.copy(out=bias_all[:], in_=bias_sum[:])
+        d_all = []
+        for b in range(B):
+            inv_root = work.tile([P, TILES, P], F32)
+            nc.vector.reciprocal(out=inv_root[:], in_=roots[b][:])
+            d_b = keep.tile([P, TILES, P], F32, name="d_all%d" % b)
+            nc.vector.scalar_tensor_tensor(
+                out=d_b[:], in0=c_sums[b], scalar=0.0, in1=inv_root[:],
+                op0=ALU.is_gt, op1=ALU.mult,
+            )
+            d_all.append(d_b)
+
+        w_codes = keep.tile([P, PASSES, H], U32, align_bytes=64)
+        w_scales = keep.tile([P, PASSES, H], U8, align_bytes=64)
+        a_flat = [keep.tile([P, TILES, N], BF16, name="a_flat%d" % b) for b in range(B)]
+        z_flat = [keep.tile([P, TILES, H], BF16, name="z_flat%d" % b) for b in range(B)]
+        a_codes = [keep.tile([P, N], U32, name="a_codes%d" % b, align_bytes=64) for b in range(B)]
+        a_scales = [keep.tile([P, N], U8, name="a_scales%d" % b, align_bytes=64) for b in range(B)]
+        z_codes = [keep.tile([P, H], U32, name="z_codes%d" % b, align_bytes=64) for b in range(B)]
+        z_scales = [keep.tile([P, H], U8, name="z_scales%d" % b, align_bytes=64) for b in range(B)]
+
+        def regroup(flat):
+            grouped = grp_pool.tile([P, H * PACK], BF16, align_bytes=64)
+            by_col = grouped[:].rearrange("p (c t) -> p c t", t=PACK)
+            split = H - SCALAR_COLS
+            nc.vector.tensor_copy(
+                out=by_col[:, :split, :].rearrange("p (c i) t -> p c t i", i=4),
+                in_=flat[:, :, :split].rearrange("p t (c i) -> p c t i", i=4),
+            )
+            nc.scalar.copy(
+                out=by_col[:, split:, :].rearrange("p (c i) t -> p c t i", i=4),
+                in_=flat[:, :, split:].rearrange("p t (c i) -> p c t i", i=4),
+            )
+            return grouped
+
+        def quantise(grouped, codes, scales):
+            nc.vector.quantize_mx(out=codes.bitcast(FP8X4), scales=scales, in_=grouped[:])
+
+        def transpose_round(j):
+            x_words = x_raw_of[j][:].bitcast(F32)
+            x_grouped = xgrp_pool.tile([P, ROUND_K], BF16, align_bytes=64)
+            grouped_words = x_grouped[:].bitcast(F32).rearrange(
+                "p (blk g r u) -> p blk g r u", blk=BLOCKS, g=2, u=2
+            )
+            for blk in range(BLOCKS):
+                x_t = tr.tile([P, 2, 2, P], F32, tag="tr")
+                for g in range(2):
+                    for u in range(2):
+                        first = ((blk * 2 + g) * 2 + u) * P
+                        nc.tensor.transpose(x_t[:, g, u, :], x_words[:, first : first + P], ident[:])
+                nc.scalar.copy(out=grouped_words[:, blk], in_=x_t[:].rearrange("p g u r -> p g r u"))
+            return x_grouped
+
+        def quantise_round(x_grouped):
+            x_codes = xq_pool.tile([P, ROUND_K // PACK], U32, align_bytes=64)
+            x_scales = xq_pool.tile([P, ROUND_K // PACK], U8, align_bytes=64)
+            half = ROUND_K // 2
+            for h in range(2):
+                words = slice(h * half // PACK, (h + 1) * half // PACK)
+                nc.vector.quantize_mx(
+                    out=x_codes[:, words].bitcast(FP8X4),
+                    scales=x_scales[:, words],
+                    in_=x_grouped[:, h * half : (h + 1) * half],
+                )
+            return x_codes, x_scales
+
+        z_acc = {}
+
+        def multiply_round(j, x_codes, x_scales):
+            batch = j // ROUNDS
+            for blk, (t, pair) in enumerate(blocks_of_round(j)):
+                for g2 in range(2):
+                    g = 2 * pair + g2
+                    if g == 0:
+                        z_acc[t] = acc.tile([P, H], F32, tag="acc", name="z_acc")
+                    nodes = slice((blk * 2 + g2) * P, (blk * 2 + g2 + 1) * P)
+                    nc.tensor.matmul_mx(
+                        out=z_acc[t][:],
+                        lhsT=x_codes[:, nodes].bitcast(FP8X4),
+                        lhsT_scale=x_scales[:, nodes],
+                        rhs=w_codes[:, g, :].bitcast(FP8X4),
+                        rhs_scale=w_scales[:, g, :],
+                        start=(g == 0),
+                        stop=(g == PASSES - 1),
+                    )
+                if pair == PAIRS - 1:
+                    if t % 2 == 0:
+                        nc.scalar.copy(out=z_flat[batch][:, t, :], in_=z_acc[t][:])
+                    else:
+                        nc.vector.tensor_copy(out=z_flat[batch][:, t, :], in_=z_acc[t][:])
+                    if t == TILES - 1:
+                        quantise(regroup(z_flat[batch]), z_codes[batch][:], z_scales[batch][:])
+
+        def quarter_of_a(b, t):
+            d_t = tr.tile([P, P], F32, tag="tr")
+            nc.tensor.transpose(d_t[:], d_all[b][:, t, :], ident[:])
+            d_col = work.tile([P, 1], F32)
+            nc.vector.tensor_copy(out=d_col[:], in_=d_t[:, 0:1])
+            nc.vector.scalar_tensor_tensor(
+                out=a_flat[b][:, t, :].rearrange("p (q s) -> p q s", s=TILES),
+                in0=adj_rows[b][:, t, :].rearrange("p (q s) -> p q s", s=TILES),
+                scalar=d_col[:],
+                in1=d_all[b][:].rearrange("p s q -> p q s"),
+                op0=ALU.mult,
+                op1=ALU.mult,
+            )
+            if t == TILES - 1:
+                quantise(regroup(a_flat[b]), a_codes[b][:], a_scales[b][:])
+
+        def second_stage(b):
+            for it in range(TILES):
+                rows = slice(it * P, (it + 1) * P)
+                o_acc = acc.tile([P, H], F32, tag="acc")
+                nc.tensor.matmul_mx(
+                    out=o_acc[:],
+                    lhsT=a_codes[b][:, rows].bitcast(FP8X4),
+                    lhsT_scale=a_scales[b][:, rows],
+                    rhs=z_codes[b][:].bitcast(FP8X4),
+                    rhs_scale=z_scales[b][:],
+                    start=True,
+                    stop=True,
+                )
+                biased = outp.tile([P, H], F32)
+                nc.vector.tensor_tensor(out=biased[:], in0=o_acc[:], in1=bias_all[:], op=ALU.add)
+                result = outp.tile([P, H], F32)
+                nc.scalar.activation(out=result[:], in_=biased[:], func=ACT.Relu)
+                nc.sync.dma_start(out=out[b, rows, :], in_=result[:])
+
+        quantised = {}
+        for j in range(B * ROUNDS + 1):
+            streaming_w = j < ROUNDS
+            if j < B * ROUNDS:
+                x_grouped = transpose_round(j)
+                if streaming_w:
+                    w_grouped = [regroup(w_raw_of[g]) for g in (2 * j, 2 * j + 1)]
+                quantised[j] = quantise_round(x_grouped)
+                if streaming_w:
+                    for g2 in range(2):
+                        g = 2 * j + g2
+                        quantise(w_grouped[g2], w_codes[:, g, :], w_scales[:, g, :])
+                else:
+                    quarter_of_a(*divmod(j - ROUNDS, TILES))
+            if j >= 1:
+                multiply_round(j - 1, *quantised[j - 1])
+                done_quarters = j - ROUNDS
+                if done_quarters > 0 and done_quarters % TILES == 0:
+                    second_stage(done_quarters // TILES - 1)

@@ -9,7 +9,6 @@ U32 = mybir.dt.uint32
 U8 = mybir.dt.uint8
 FP8X4 = mybir.dt.float8_e4m3fn_x4
 ALU = mybir.AluOpType
-ACT = mybir.ActivationFunctionType
 
 B, N, D, H = 2, 512, 8192, 512
 FLOPS = 2 * B * N * D * H + 2 * B * N * N * H
@@ -46,7 +45,7 @@ def tile_perception_pa_k_kernel(tc, batch_graph, adj, W1, b1, out):
         wraw_pool = ctx.enter_context(tc.tile_pool(name="wraw", bufs=4))
         grp_pool = ctx.enter_context(tc.tile_pool(name="grp", bufs=3))
         work = ctx.enter_context(tc.tile_pool(name="work", bufs=2))
-        outp = ctx.enter_context(tc.tile_pool(name="outp", bufs=3))
+        outp = ctx.enter_context(tc.tile_pool(name="outp", bufs=TILES))
         acc = ctx.enter_context(tc.psum_pool(name="acc", bufs=4))
         tr = ctx.enter_context(tc.psum_pool(name="tr", bufs=BLOCKS))
 
@@ -134,18 +133,19 @@ def tile_perception_pa_k_kernel(tc, batch_graph, adj, W1, b1, out):
         z_codes = [keep.tile([P, H], U32, name="z_codes%d" % b, align_bytes=64) for b in range(B)]
         z_scales = [keep.tile([P, H], U8, name="z_scales%d" % b, align_bytes=64) for b in range(B)]
 
-        def regroup(flat):
+        def regroup(flat, scalar_cols):
             grouped = grp_pool.tile([P, H * PACK], BF16, align_bytes=64)
             by_col = grouped[:].rearrange("p (c t) -> p c t", t=PACK)
-            split = H - SCALAR_COLS
+            split = H - scalar_cols
             nc.vector.tensor_copy(
                 out=by_col[:, :split, :].rearrange("p (c i) t -> p c t i", i=4),
                 in_=flat[:, :, :split].rearrange("p t (c i) -> p c t i", i=4),
             )
-            nc.scalar.copy(
-                out=by_col[:, split:, :].rearrange("p (c i) t -> p c t i", i=4),
-                in_=flat[:, :, split:].rearrange("p t (c i) -> p c t i", i=4),
-            )
+            if scalar_cols > 0:
+                nc.scalar.copy(
+                    out=by_col[:, split:, :].rearrange("p (c i) t -> p c t i", i=4),
+                    in_=flat[:, :, split:].rearrange("p t (c i) -> p c t i", i=4),
+                )
             return grouped
 
         def quantise(grouped, codes, scales):
@@ -199,28 +199,21 @@ def tile_perception_pa_k_kernel(tc, batch_graph, adj, W1, b1, out):
                         stop=(g == PASSES - 1),
                     )
                 if pair == PAIRS - 1:
-                    if t % 2 == 0:
-                        nc.scalar.copy(out=z_flat[batch][:, t, :], in_=z_acc[t][:])
-                    else:
-                        nc.vector.tensor_copy(out=z_flat[batch][:, t, :], in_=z_acc[t][:])
+                    nc.scalar.copy(out=z_flat[batch][:, t, :], in_=z_acc[t][:])
                     if t == TILES - 1:
-                        quantise(regroup(z_flat[batch]), z_codes[batch][:], z_scales[batch][:])
+                        quantise(regroup(z_flat[batch], 0), z_codes[batch][:], z_scales[batch][:])
 
         def quarter_of_a(b, t):
-            d_t = tr.tile([P, P], F32, tag="tr")
-            nc.tensor.transpose(d_t[:], d_all[b][:, t, :], ident[:])
-            d_col = work.tile([P, 1], F32)
-            nc.vector.tensor_copy(out=d_col[:], in_=d_t[:, 0:1])
             nc.vector.scalar_tensor_tensor(
                 out=a_flat[b][:, t, :].rearrange("p (q s) -> p q s", s=TILES),
                 in0=adj_rows[b][:, t, :].rearrange("p (q s) -> p q s", s=TILES),
-                scalar=d_col[:],
+                scalar=d_cols[b][:, t : t + 1],
                 in1=d_all[b][:].rearrange("p s q -> p q s"),
                 op0=ALU.mult,
                 op1=ALU.mult,
             )
             if t == TILES - 1:
-                quantise(regroup(a_flat[b]), a_codes[b][:], a_scales[b][:])
+                quantise(regroup(a_flat[b], 0), a_codes[b][:], a_scales[b][:])
 
         def second_stage(b):
             for it in range(TILES):
@@ -238,25 +231,37 @@ def tile_perception_pa_k_kernel(tc, batch_graph, adj, W1, b1, out):
                 biased = outp.tile([P, H], F32)
                 nc.vector.tensor_tensor(out=biased[:], in0=o_acc[:], in1=bias_all[:], op=ALU.add)
                 result = outp.tile([P, H], F32)
-                nc.scalar.activation(out=result[:], in_=biased[:], func=ACT.Relu)
+                nc.gpsimd.tensor_scalar(
+                    out=result[:], in0=biased[:], scalar1=0.0, scalar2=0.0, op0=ALU.max, op1=ALU.add
+                )
                 nc.sync.dma_start(out=out[b, rows, :], in_=result[:])
 
-        quantised = {}
-        for j in range(B * ROUNDS + 1):
-            streaming_w = j < ROUNDS
-            if j < B * ROUNDS:
-                x_grouped = transpose_round(j)
-                if streaming_w:
-                    w_grouped = [regroup(w_raw_of[g]) for g in (2 * j, 2 * j + 1)]
-                quantised[j] = quantise_round(x_grouped)
-                if streaming_w:
-                    for g2 in range(2):
-                        g = 2 * j + g2
-                        quantise(w_grouped[g2], w_codes[:, g, :], w_scales[:, g, :])
-                else:
-                    quarter_of_a(*divmod(j - ROUNDS, TILES))
-            if j >= 1:
-                multiply_round(j - 1, *quantised[j - 1])
-                done_quarters = j - ROUNDS
-                if done_quarters > 0 and done_quarters % TILES == 0:
-                    second_stage(done_quarters // TILES - 1)
+        def prepare_round(j):
+            x_grouped = transpose_round(j)
+            if j < ROUNDS:
+                w_grouped = [regroup(w_raw_of[g], SCALAR_COLS) for g in (2 * j, 2 * j + 1)]
+            codes_and_scales = quantise_round(x_grouped)
+            if j < ROUNDS:
+                for g2 in range(2):
+                    g = 2 * j + g2
+                    quantise(w_grouped[g2], w_codes[:, g, :], w_scales[:, g, :])
+            else:
+                quarter_of_a(*divmod(j - ROUNDS, TILES))
+            return codes_and_scales
+
+        ready = prepare_round(0)
+        d_cols = []
+        for b in range(B):
+            d_t = tr.tile([P, TILES, P], F32, tag="tr")
+            for t in range(TILES):
+                nc.tensor.transpose(d_t[:, t, :], d_all[b][:, t, :], ident[:])
+            d_col = keep.tile([P, TILES], F32, name="d_col%d" % b)
+            nc.vector.tensor_copy(out=d_col[:], in_=d_t[:, :, 0])
+            d_cols.append(d_col)
+        for j in range(B * ROUNDS):
+            following = prepare_round(j + 1) if j + 1 < B * ROUNDS else None
+            multiply_round(j, *ready)
+            ready = following
+            quarters_done = j + 1 - ROUNDS
+            if quarters_done > 0 and quarters_done % TILES == 0:
+                second_stage(quarters_done // TILES - 1)

@@ -9,6 +9,7 @@ U32 = mybir.dt.uint32
 U8 = mybir.dt.uint8
 FP8X4 = mybir.dt.float8_e4m3fn_x4
 ALU = mybir.AluOpType
+ACT = mybir.ActivationFunctionType
 
 B, N, D, H = 2, 512, 8192, 512
 FLOPS = 2 * B * N * D * H + 2 * B * N * N * H
@@ -22,16 +23,27 @@ PAIR_K = 2 * K_PASS
 PAIRS = PASSES // 2
 BLOCKS = 4
 ROUND_K = BLOCKS * PAIR_K
-ROUNDS = TILES * PAIRS // BLOCKS
+HALF = PAIRS // 2
+ROUNDS = B * TILES * PAIRS // BLOCKS
+LAST_OF_GRAPH_1 = HALF + PAIRS - 1
+SECOND_STAGE_LAG = 2
 SCALAR_COLS = 128
 
 
-def blocks_of_round(j):
-    batch, r = divmod(j, ROUNDS)
-    if batch == 0:
-        return [(blk, r) for blk in range(BLOCKS)]
-    rounds_per_tile = PAIRS // BLOCKS
-    return [(r // rounds_per_tile, BLOCKS * (r % rounds_per_tile) + blk) for blk in range(BLOCKS)]
+def plan_of_round(j):
+    if j < HALF:
+        return 0, 0, PASSES // 2 - 1, [(blk, j) for blk in range(BLOCKS)]
+    if j <= LAST_OF_GRAPH_1:
+        return 1, 0, PASSES - 1, [(blk, j - HALF) for blk in range(BLOCKS)]
+    return 0, PASSES // 2, PASSES - 1, [(j - LAST_OF_GRAPH_1 - 1, HALF + blk) for blk in range(BLOCKS)]
+
+
+def w_passes_of_round(j):
+    if j < HALF:
+        return [2 * j, 2 * j + 1]
+    if j < HALF + PASSES // 2:
+        return [PASSES // 2 + j - HALF]
+    return []
 
 
 def tile_perception_pa_k_kernel(tc, batch_graph, adj, W1, b1, out):
@@ -65,13 +77,13 @@ def tile_perception_pa_k_kernel(tc, batch_graph, adj, W1, b1, out):
 
         w_view = W1.rearrange("(g u q e) c -> g q u e c", u=2, q=P, e=2)
         x_raw_of = []
-        w_raw_of = []
-        for j in range(B * ROUNDS):
-            batch = j // ROUNDS
-            x_view = batch_graph[batch].rearrange("(p t) k -> p t k", t=TILES)
-            first_tile, first_pair = blocks_of_round(j)[0]
+        w_raw_of = {}
+        for j in range(ROUNDS):
+            graph, first_pass, last_pass, blocks = plan_of_round(j)
+            x_view = batch_graph[graph].rearrange("(p t) k -> p t k", t=TILES)
+            first_tile, first_pair = blocks[0]
             x_raw = xraw_pool.tile([P, ROUND_K], BF16)
-            if batch == 0:
+            if blocks[1][0] != first_tile:
                 nc.sync.dma_start(
                     out=x_raw[:].rearrange("p (t k) -> p t k", t=TILES),
                     in_=x_view[:, :, first_pair * PAIR_K : (first_pair + 1) * PAIR_K],
@@ -82,13 +94,10 @@ def tile_perception_pa_k_kernel(tc, batch_graph, adj, W1, b1, out):
                     in_=x_view[:, first_tile, first_pair * PAIR_K : first_pair * PAIR_K + ROUND_K],
                 )
             x_raw_of.append(x_raw)
-            if batch == 0:
-                for g in (2 * j, 2 * j + 1):
-                    w_raw = wraw_pool.tile([P, PACK, H], BF16)
-                    nc.sync.dma_start(
-                        out=w_raw[:].rearrange("q (u e) c -> q u e c", u=2), in_=w_view[g]
-                    )
-                    w_raw_of.append(w_raw)
+            for g in w_passes_of_round(j):
+                w_raw = wraw_pool.tile([P, PACK, H], BF16)
+                nc.sync.dma_start(out=w_raw[:].rearrange("q (u e) c -> q u e c", u=2), in_=w_view[g])
+                w_raw_of[g] = w_raw
 
         c_sums = []
         c_floors = []
@@ -128,6 +137,7 @@ def tile_perception_pa_k_kernel(tc, batch_graph, adj, W1, b1, out):
         w_scales = keep.tile([P, PASSES, H], U8, align_bytes=64)
         a_flat = [keep.tile([P, TILES, N], BF16, name="a_flat%d" % b) for b in range(B)]
         z_flat = [keep.tile([P, TILES, H], BF16, name="z_flat%d" % b) for b in range(B)]
+        z_part = [keep.tile([P, H], F32, name="z_part%d" % t) for t in range(TILES)]
         a_codes = [keep.tile([P, N], U32, name="a_codes%d" % b, align_bytes=64) for b in range(B)]
         a_scales = [keep.tile([P, N], U8, name="a_scales%d" % b, align_bytes=64) for b in range(B)]
         z_codes = [keep.tile([P, H], U32, name="z_codes%d" % b, align_bytes=64) for b in range(B)]
@@ -182,11 +192,11 @@ def tile_perception_pa_k_kernel(tc, batch_graph, adj, W1, b1, out):
         z_acc = {}
 
         def multiply_round(j, x_codes, x_scales):
-            batch = j // ROUNDS
-            for blk, (t, pair) in enumerate(blocks_of_round(j)):
+            graph, first_pass, last_pass, blocks = plan_of_round(j)
+            for blk, (t, pair) in enumerate(blocks):
                 for g2 in range(2):
                     g = 2 * pair + g2
-                    if g == 0:
+                    if g == first_pass:
                         z_acc[t] = acc.tile([P, H], F32, tag="acc", name="z_acc")
                     nodes = slice((blk * 2 + g2) * P, (blk * 2 + g2 + 1) * P)
                     nc.tensor.matmul_mx(
@@ -195,13 +205,25 @@ def tile_perception_pa_k_kernel(tc, batch_graph, adj, W1, b1, out):
                         lhsT_scale=x_scales[:, nodes],
                         rhs=w_codes[:, g, :].bitcast(FP8X4),
                         rhs_scale=w_scales[:, g, :],
-                        start=(g == 0),
-                        stop=(g == PASSES - 1),
+                        start=(g == first_pass),
+                        stop=(g == last_pass),
                     )
-                if pair == PAIRS - 1:
-                    nc.scalar.copy(out=z_flat[batch][:, t, :], in_=z_acc[t][:])
-                    if t == TILES - 1:
-                        quantise(regroup(z_flat[batch], 0), z_codes[batch][:], z_scales[batch][:])
+                if 2 * pair + 1 != last_pass:
+                    continue
+                if last_pass != PASSES - 1:
+                    if t % 2 == 0:
+                        nc.scalar.copy(out=z_part[t][:], in_=z_acc[t][:])
+                    else:
+                        nc.vector.tensor_copy(out=z_part[t][:], in_=z_acc[t][:])
+                    continue
+                if first_pass == 0:
+                    nc.scalar.copy(out=z_flat[graph][:, t, :], in_=z_acc[t][:])
+                else:
+                    nc.vector.tensor_tensor(
+                        out=z_flat[graph][:, t, :], in0=z_acc[t][:], in1=z_part[t][:], op=ALU.add
+                    )
+                if t == TILES - 1:
+                    quantise(regroup(z_flat[graph], 0), z_codes[graph][:], z_scales[graph][:])
 
         def quarter_of_a(b, t):
             nc.vector.scalar_tensor_tensor(
@@ -215,7 +237,8 @@ def tile_perception_pa_k_kernel(tc, batch_graph, adj, W1, b1, out):
             if t == TILES - 1:
                 quantise(regroup(a_flat[b], 0), a_codes[b][:], a_scales[b][:])
 
-        def second_stage(b):
+        def multiply_second(b):
+            sums = []
             for it in range(TILES):
                 rows = slice(it * P, (it + 1) * P)
                 o_acc = acc.tile([P, H], F32, tag="acc")
@@ -230,23 +253,23 @@ def tile_perception_pa_k_kernel(tc, batch_graph, adj, W1, b1, out):
                 )
                 biased = outp.tile([P, H], F32)
                 nc.vector.tensor_tensor(out=biased[:], in0=o_acc[:], in1=bias_all[:], op=ALU.add)
+                sums.append(biased)
+            return sums
+
+        def relu_and_store(b, sums):
+            for it in range(TILES):
                 result = outp.tile([P, H], F32)
-                nc.gpsimd.tensor_scalar(
-                    out=result[:], in0=biased[:], scalar1=0.0, scalar2=0.0, op0=ALU.max, op1=ALU.add
-                )
-                nc.sync.dma_start(out=out[b, rows, :], in_=result[:])
+                nc.scalar.activation(out=result[:], in_=sums[it][:], func=ACT.Relu)
+                nc.sync.dma_start(out=out[b, it * P : (it + 1) * P, :], in_=result[:])
 
         def prepare_round(j):
             x_grouped = transpose_round(j)
-            if j < ROUNDS:
-                w_grouped = [regroup(w_raw_of[g], SCALAR_COLS) for g in (2 * j, 2 * j + 1)]
+            w_grouped = [regroup(w_raw_of[g], SCALAR_COLS) for g in w_passes_of_round(j)]
             codes_and_scales = quantise_round(x_grouped)
-            if j < ROUNDS:
-                for g2 in range(2):
-                    g = 2 * j + g2
-                    quantise(w_grouped[g2], w_codes[:, g, :], w_scales[:, g, :])
-            else:
-                quarter_of_a(*divmod(j - ROUNDS, TILES))
+            for g, grouped in zip(w_passes_of_round(j), w_grouped):
+                quantise(grouped, w_codes[:, g, :], w_scales[:, g, :])
+            if HALF <= j < HALF + B * TILES:
+                quarter_of_a(*divmod(j - HALF, TILES))
             return codes_and_scales
 
         ready = prepare_round(0)
@@ -258,10 +281,12 @@ def tile_perception_pa_k_kernel(tc, batch_graph, adj, W1, b1, out):
             d_col = keep.tile([P, TILES], F32, name="d_col%d" % b)
             nc.vector.tensor_copy(out=d_col[:], in_=d_t[:, :, 0])
             d_cols.append(d_col)
-        for j in range(B * ROUNDS):
-            following = prepare_round(j + 1) if j + 1 < B * ROUNDS else None
+        for j in range(ROUNDS):
+            following = prepare_round(j + 1) if j + 1 < ROUNDS else None
+            if j == LAST_OF_GRAPH_1 + SECOND_STAGE_LAG + 1:
+                relu_and_store(1, sums_of_graph_1)
             multiply_round(j, *ready)
             ready = following
-            quarters_done = j + 1 - ROUNDS
-            if quarters_done > 0 and quarters_done % TILES == 0:
-                second_stage(quarters_done // TILES - 1)
+            if j == LAST_OF_GRAPH_1 + SECOND_STAGE_LAG:
+                sums_of_graph_1 = multiply_second(1)
+        relu_and_store(0, multiply_second(0))

@@ -31,11 +31,16 @@ SCALAR_COLS = 128
 
 
 def plan_of_round(j):
-    if j < HALF:
-        return 0, 0, PASSES // 2 - 1, [(blk, j) for blk in range(BLOCKS)]
-    if j <= LAST_OF_GRAPH_1:
-        return 1, 0, PASSES - 1, [(blk, j - HALF) for blk in range(BLOCKS)]
-    return 0, PASSES // 2, PASSES - 1, [(j - LAST_OF_GRAPH_1 - 1, HALF + blk) for blk in range(BLOCKS)]
+    stretch, r = divmod(j, HALF)
+    together = [(blk, HALF * (stretch // 2) + r) for blk in range(BLOCKS)]
+    one_tile = [(r, HALF * (stretch // 2) + blk) for blk in range(BLOCKS)]
+    if stretch == 0:
+        return 0, 0, PASSES // 2 - 1, together
+    if stretch == 1:
+        return 1, 0, PASSES - 1, one_tile
+    if stretch == 2:
+        return 1, 0, PASSES - 1, together
+    return 0, PASSES // 2, PASSES - 1, one_tile
 
 
 def w_passes_of_round(j):

@@ -21,34 +21,36 @@ PASSES = D // K_PASS
 TILES = N // P
 PAIR_K = 2 * K_PASS
 PAIRS = PASSES // 2
-BLOCKS = 4
-ROUND_K = BLOCKS * PAIR_K
 HALF = PAIRS // 2
-ROUNDS = B * TILES * PAIRS // BLOCKS
-LAST_OF_GRAPH_1 = HALF + PAIRS - 1
-SECOND_STAGE_LAG = 2
-SCALAR_COLS = 128
+
+HEAD = [(0, 0), (0, 1), (0, 2), (1, 0), (1, 1)]
+ROUNDS = (
+    [[(b, t, pair) for b, t in HEAD] for pair in range(HALF)]
+    + [[(1, t, pair) for pair in range(HALF)] for t in (2, 3)]
+    + [[(1, t, pair) for t in range(TILES)] for pair in range(HALF, PAIRS)]
+    + [[(0, t, pair) for pair in range(HALF, PAIRS)] for t in range(3)]
+    + [[(0, 3, pair) for pair in range(HALF)], [(0, 3, pair) for pair in range(HALF, PAIRS)]]
+)
+LAST = len(ROUNDS) - 1
+W_OF_ROUND = {0: [0, 1], 1: [2, 3], 2: [4, 5], 3: [6, 7], 5: [8, 9], 6: [10], 7: [11, 12], 8: [13, 14], 9: [15]}
+LOADS = ["x1", "w2", "w3", "x2", "w4", "w5", "x3", "w6", "w7", "x4", "x5", "w8", "w9", "x6", "w10", "x7", "w11", "w12", "x8", "adj", "w13", "w14", "x9", "w15", "x10", "x11", "x12", "x13", "x14"]
+ACC_BANK = {(0, 0, 0): 0, (0, 1, 0): 1, (0, 2, 0): 2, (1, 0, 0): 3, (1, 1, 0): 4, (1, 2, 0): 0, (1, 3, 0): 1,
+            (0, 0, 1): 3, (0, 1, 1): 4, (0, 2, 1): 3}
+OUT_BANK_1 = [1, 0, 1, 0]
+LAST_BANK = [4, 3]
+OUT_BANK_0 = [1, 0, 2, 5, 6, 7]
+C_AT = 7
+A_AT = {8: [(1, 0), (1, 1), (1, 2), (1, 3)], 9: [(1, 4)], 10: [(1, 5)], 11: [(0, 0), (0, 1), (0, 2), (0, 3)], 12: [(0, 4)], 13: [(0, 5)]}
+SECOND_AFTER = {12: [0, 1], 13: [2, 3]}
+LAST_PARTS = [(0, 256), (256, 512)]
+LAST_SHARE = 64
+HEAD_SHARE = 128
+SHARE = 128
+EARLY = {3: 5}
 
 
-def plan_of_round(j):
-    stretch, r = divmod(j, HALF)
-    together = [(blk, HALF * (stretch // 2) + r) for blk in range(BLOCKS)]
-    one_tile = [(r, HALF * (stretch // 2) + blk) for blk in range(BLOCKS)]
-    if stretch == 0:
-        return 0, 0, PASSES // 2 - 1, together
-    if stretch == 1:
-        return 1, 0, PASSES - 1, one_tile
-    if stretch == 2:
-        return 1, 0, PASSES - 1, together
-    return 0, PASSES // 2, PASSES - 1, one_tile
-
-
-def w_passes_of_round(j):
-    if j < HALF:
-        return [2 * j, 2 * j + 1]
-    if j < HALF + PASSES // 2:
-        return [PASSES // 2 + j - HALF]
-    return []
+def tr_banks(j):
+    return [5, 6, 7] if j <= HALF else [2, 5, 6, 7]
 
 
 def tile_perception_pa_k_kernel(tc, batch_graph, adj, W1, b1, out):
@@ -56,15 +58,16 @@ def tile_perception_pa_k_kernel(tc, batch_graph, adj, W1, b1, out):
     with ExitStack() as ctx:
         ctx.enter_context(tc.manual_schedule())
         keep = ctx.enter_context(tc.tile_pool(name="keep", bufs=1))
-        xraw_pool = ctx.enter_context(tc.tile_pool(name="xraw", bufs=5))
-        xgrp_pool = ctx.enter_context(tc.tile_pool(name="xgrp", bufs=3))
+        xraw_pool = ctx.enter_context(tc.tile_pool(name="xraw", bufs=4))
+        xgrp_pool = ctx.enter_context(tc.tile_pool(name="xgrp", bufs=2))
         xq_pool = ctx.enter_context(tc.tile_pool(name="xq", bufs=3))
         wraw_pool = ctx.enter_context(tc.tile_pool(name="wraw", bufs=4))
         grp_pool = ctx.enter_context(tc.tile_pool(name="grp", bufs=3))
-        work = ctx.enter_context(tc.tile_pool(name="work", bufs=2))
-        outp = ctx.enter_context(tc.tile_pool(name="outp", bufs=TILES))
-        acc = ctx.enter_context(tc.psum_pool(name="acc", bufs=4))
-        tr = ctx.enter_context(tc.psum_pool(name="tr", bufs=BLOCKS))
+        outp = ctx.enter_context(tc.tile_pool(name="outp", bufs=4))
+        psum = ctx.enter_context(tc.psum_pool(name="psum", bufs=1))
+
+        def bank(i, shape):
+            return psum.tile(shape, F32, tag="bank%d" % i, name="bank")
 
         ident = keep.tile([P, P], F32)
         make_identity(nc, ident[:])
@@ -72,86 +75,80 @@ def tile_perception_pa_k_kernel(tc, batch_graph, adj, W1, b1, out):
         nc.vector.memset(ones[:], 1.0)
         bias_rows = keep.tile([P, H], BF16)
         nc.vector.memset(bias_rows[:], 0.0)
+        floor_col = keep.tile([P, 1], F32)
+        nc.vector.memset(floor_col[:], 1e-30)
+        warm = keep.tile([P, 1], F32)
+        nc.scalar.activation(out=warm[:], in_=ones[:, 0:1], func=ACT.Abs_reciprocal_sqrt)
 
         adj_rows = []
-        for b in range(B):
-            adj_b = keep.tile([P, TILES, N], BF16, name="adj_rows%d" % b)
-            nc.sync.dma_start(out=adj_b[:], in_=adj[b].rearrange("(p t) i -> p t i", t=TILES))
-            adj_rows.append(adj_b)
-        nc.sync.dma_start(out=bias_rows[0:1, :], in_=b1.unsqueeze(0))
+
+        def load_adj_and_bias():
+            for b in range(B):
+                adj_b = keep.tile([P, TILES, N], BF16, name="adj_rows%d" % b)
+                nc.sync.dma_start(out=adj_b[:], in_=adj[b].rearrange("(p t) i -> p t i", t=TILES))
+                adj_rows.append(adj_b)
+            nc.sync.dma_start(out=bias_rows[0:1, :], in_=b1.unsqueeze(0))
 
         w_view = W1.rearrange("(g u q e) c -> g q u e c", u=2, q=P, e=2)
-        x_raw_of = []
+        x_views = [batch_graph[b].rearrange("(p t) k -> p t k", t=TILES) for b in range(B)]
+        x_raw_of = {}
         w_raw_of = {}
-        for j in range(ROUNDS):
-            graph, first_pass, last_pass, blocks = plan_of_round(j)
-            x_view = batch_graph[graph].rearrange("(p t) k -> p t k", t=TILES)
-            first_tile, first_pair = blocks[0]
-            x_raw = xraw_pool.tile([P, ROUND_K], BF16)
-            if blocks[1][0] != first_tile:
-                nc.sync.dma_start(
-                    out=x_raw[:].rearrange("p (t k) -> p t k", t=TILES),
-                    in_=x_view[:, :, first_pair * PAIR_K : (first_pair + 1) * PAIR_K],
-                )
+
+        def load_w(g):
+            w_raw = wraw_pool.tile([P, PACK, H], BF16)
+            nc.sync.dma_start(out=w_raw[:].rearrange("q (u e) c -> q u e c", u=2), in_=w_view[g])
+            w_raw_of[g] = w_raw
+
+        def load_x_blocks(j, first, last):
+            b, t, pair = ROUNDS[j][first]
+            n = last - first + 1
+            dst = x_raw_of[j][:, first * PAIR_K : (last + 1) * PAIR_K]
+            if n > 1 and ROUNDS[j][first + 1][1] == t:
+                nc.sync.dma_start(out=dst, in_=x_views[b][:, t, pair * PAIR_K : (pair + n) * PAIR_K])
             else:
                 nc.sync.dma_start(
-                    out=x_raw[:],
-                    in_=x_view[:, first_tile, first_pair * PAIR_K : first_pair * PAIR_K + ROUND_K],
+                    out=dst.rearrange("p (t k) -> p t k", t=n),
+                    in_=x_views[b][:, t : t + n, pair * PAIR_K : (pair + 1) * PAIR_K],
                 )
-            x_raw_of.append(x_raw)
-            for g in w_passes_of_round(j):
-                w_raw = wraw_pool.tile([P, PACK, H], BF16)
-                nc.sync.dma_start(out=w_raw[:].rearrange("q (u e) c -> q u e c", u=2), in_=w_view[g])
-                w_raw_of[g] = w_raw
 
-        c_sums = []
-        c_floors = []
-        for b in range(B):
-            c_sum = acc.tile([P, N], F32, tag="acc")
-            for t in range(TILES):
-                nc.tensor.matmul(
-                    out=c_sum[:], lhsT=ones[:], rhs=adj_rows[b][:, t, :],
-                    start=(t == 0), stop=(t == TILES - 1),
-                )
-            c_by_tile = c_sum[:].rearrange("m (q t) -> m t q", t=TILES)
-            c_floor = work.tile([P, TILES, P], F32)
-            nc.vector.tensor_scalar_max(out=c_floor[:], in0=c_by_tile, scalar1=1e-30)
-            c_sums.append(c_by_tile)
-            c_floors.append(c_floor)
-        bias_sum = acc.tile([P, H], F32, tag="acc")
-        nc.tensor.matmul(out=bias_sum[:], lhsT=ones[:], rhs=bias_rows[:], start=True, stop=True)
-        roots = []
-        for b in range(B):
-            root = work.tile([P, TILES, P], F32)
-            nc.scalar.sqrt(out=root[:], in_=c_floors[b][:])
-            roots.append(root)
-        bias_all = keep.tile([P, H], F32)
-        nc.scalar.copy(out=bias_all[:], in_=bias_sum[:])
-        d_all = []
-        for b in range(B):
-            inv_root = work.tile([P, TILES, P], F32)
-            nc.vector.reciprocal(out=inv_root[:], in_=roots[b][:])
-            d_b = keep.tile([P, TILES, P], F32, name="d_all%d" % b)
-            nc.vector.scalar_tensor_tensor(
-                out=d_b[:], in0=c_sums[b], scalar=0.0, in1=inv_root[:],
-                op0=ALU.is_gt, op1=ALU.mult,
-            )
-            d_all.append(d_b)
+        def new_x(j):
+            x_raw_of[j] = xraw_pool.tile([P, len(HEAD) * PAIR_K], BF16, name="x_raw")
+
+        new_x(0)
+        load_x_blocks(0, 0, 0)
+        load_x_blocks(0, 1, 2)
+        load_w(0)
+        load_x_blocks(0, 3, 4)
+        load_w(1)
+        for what in LOADS:
+            if what == "adj":
+                load_adj_and_bias()
+            elif what[0] == "w":
+                load_w(int(what[1:]))
+            else:
+                j = int(what[1:])
+                new_x(j)
+                if j < HALF:
+                    load_x_blocks(j, 0, 2)
+                    load_x_blocks(j, 3, 4)
+                else:
+                    load_x_blocks(j, 0, 3)
 
         w_codes = keep.tile([P, PASSES, H], U32, align_bytes=64)
         w_scales = keep.tile([P, PASSES, H], U8, align_bytes=64)
-        a_flat = [keep.tile([P, TILES, N], BF16, name="a_flat%d" % b) for b in range(B)]
+        dd = [keep.tile([P, TILES, N], BF16, name="dd%d" % b) for b in range(B)]
         z_flat = [keep.tile([P, TILES, H], BF16, name="z_flat%d" % b) for b in range(B)]
-        z_part = [keep.tile([P, H], F32, name="z_part%d" % t) for t in range(TILES)]
+        z_part = [keep.tile([P, H], F32, name="z_part%d" % t) for t in range(TILES - 1)]
         a_codes = [keep.tile([P, N], U32, name="a_codes%d" % b, align_bytes=64) for b in range(B)]
         a_scales = [keep.tile([P, N], U8, name="a_scales%d" % b, align_bytes=64) for b in range(B)]
         z_codes = [keep.tile([P, H], U32, name="z_codes%d" % b, align_bytes=64) for b in range(B)]
         z_scales = [keep.tile([P, H], U8, name="z_scales%d" % b, align_bytes=64) for b in range(B)]
 
         def regroup(flat, scalar_cols):
-            grouped = grp_pool.tile([P, H * PACK], BF16, align_bytes=64)
-            by_col = grouped[:].rearrange("p (c t) -> p c t", t=PACK)
-            split = H - scalar_cols
+            width = flat.shape[2]
+            grouped = grp_pool.tile([P, H * PACK], BF16, name="grouped", align_bytes=64)[:, : width * PACK]
+            by_col = grouped.rearrange("p (c t) -> p c t", t=PACK)
+            split = width - scalar_cols
             nc.vector.tensor_copy(
                 out=by_col[:, :split, :].rearrange("p (c i) t -> p c t i", i=4),
                 in_=flat[:, :, :split].rearrange("p t (c i) -> p c t i", i=4),
@@ -164,134 +161,267 @@ def tile_perception_pa_k_kernel(tc, batch_graph, adj, W1, b1, out):
             return grouped
 
         def quantise(grouped, codes, scales):
-            nc.vector.quantize_mx(out=codes.bitcast(FP8X4), scales=scales, in_=grouped[:])
+            nc.vector.quantize_mx(out=codes.bitcast(FP8X4), scales=scales, in_=grouped)
 
-        def transpose_round(j):
-            x_words = x_raw_of[j][:].bitcast(F32)
-            x_grouped = xgrp_pool.tile([P, ROUND_K], BF16, align_bytes=64)
-            grouped_words = x_grouped[:].bitcast(F32).rearrange(
-                "p (blk g r u) -> p blk g r u", blk=BLOCKS, g=2, u=2
+        d_all = []
+        d_cols = []
+        bias_all = keep.tile([P, H], F32)
+
+        def column_sums():
+            for b in range(B):
+                c_sum = bank(tr_banks(LAST)[b], [P, N])
+                for t in range(TILES):
+                    nc.tensor.matmul(
+                        out=c_sum[:], lhsT=ones[:], rhs=adj_rows[b][:, t, :],
+                        start=(t == 0), stop=(t == TILES - 1),
+                    )
+                d_b = keep.tile([P, N], F32, name="d_all%d" % b)
+                nc.scalar.activation(
+                    out=d_b[:], in_=c_sum[:], func=ACT.Abs_reciprocal_sqrt, bias=floor_col[:]
+                )
+                d_all.append(d_b)
+            bias_sum = bank(tr_banks(LAST)[2], [P, H])
+            nc.tensor.matmul(out=bias_sum[:], lhsT=ones[:], rhs=bias_rows[:], start=True, stop=True)
+            nc.scalar.copy(out=bias_all[:], in_=bias_sum[:])
+
+        def d_columns():
+            for b in range(B):
+                d_t = bank(tr_banks(LAST)[b], [P, TILES, P])
+                for t in range(TILES):
+                    nc.tensor.transpose(d_t[:, t, :], d_all[b][:, t::TILES], ident[:])
+                d_raw = keep.tile([P, TILES], F32, name="d_raw%d" % b)
+                nc.vector.tensor_copy(out=d_raw[:], in_=d_t[:, :, 0])
+                d_col = keep.tile([P, TILES], F32, name="d_col%d" % b)
+                nc.vector.scalar_tensor_tensor(
+                    out=d_col[:], in0=d_raw[:], scalar=1e14, in1=d_raw[:],
+                    op0=ALU.is_lt, op1=ALU.mult,
+                )
+                d_cols.append(d_col)
+
+        a_grouped = {}
+
+        def products_of_d(b, t):
+            nc.vector.tensor_scalar_mul(
+                out=dd[b][:, t, :], in0=d_all[b][:], scalar1=d_cols[b][:, t : t + 1]
             )
-            for blk in range(BLOCKS):
-                x_t = tr.tile([P, 2, 2, P], F32, tag="tr")
+
+        def mask_a(b):
+            grouped = grp_pool.tile([P, N * PACK], BF16, name="grouped", align_bytes=64)
+            nc.vector.tensor_tensor(
+                out=grouped[:].rearrange("p (c i t) -> p c t i", i=4, t=PACK),
+                in0=adj_rows[b][:].rearrange("p t (c i) -> p c t i", i=4),
+                in1=dd[b][:].rearrange("p t (c i) -> p c t i", i=4),
+                op=ALU.mult,
+            )
+            a_grouped[b] = grouped[:]
+
+        def quantise_a(b):
+            quantise(a_grouped[b], a_codes[b][:], a_scales[b][:])
+
+        def prepare_round(j):
+            blocks = ROUNDS[j]
+            x_grouped = xgrp_pool.tile([P, len(HEAD) * PAIR_K], BF16, align_bytes=64)
+            x_codes = xq_pool.tile([P, len(HEAD) * PAIR_K // PACK], U32, align_bytes=64)
+            x_scales = xq_pool.tile([P, len(HEAD) * PAIR_K // PACK], U8, align_bytes=64)
+            x_words = x_raw_of[j][:].bitcast(F32)
+            grouped_words = x_grouped[:].bitcast(F32).rearrange(
+                "p (blk g r u) -> p blk g r u", g=2, r=P, u=2
+            )
+            banks = tr_banks(j)
+            for blk in range(len(blocks)):
+                x_t = bank(banks[(j + blk) % len(banks)], [P, 2, 2, P])
                 for g in range(2):
                     for u in range(2):
                         first = ((blk * 2 + g) * 2 + u) * P
                         nc.tensor.transpose(x_t[:, g, u, :], x_words[:, first : first + P], ident[:])
                 nc.scalar.copy(out=grouped_words[:, blk], in_=x_t[:].rearrange("p g u r -> p g r u"))
-            return x_grouped
 
-        def quantise_round(x_grouped):
-            x_codes = xq_pool.tile([P, ROUND_K // PACK], U32, align_bytes=64)
-            x_scales = xq_pool.tile([P, ROUND_K // PACK], U8, align_bytes=64)
-            half = ROUND_K // 2
-            for h in range(2):
-                words = slice(h * half // PACK, (h + 1) * half // PACK)
-                nc.vector.quantize_mx(
-                    out=x_codes[:, words].bitcast(FP8X4),
-                    scales=x_scales[:, words],
-                    in_=x_grouped[:, h * half : (h + 1) * half],
-                )
+            def quantise_blocks(first, last):
+                values = slice(first * PAIR_K, last * PAIR_K)
+                words = slice(first * PAIR_K // PACK, last * PAIR_K // PACK)
+                quantise(x_grouped[:, values], x_codes[:, words], x_scales[:, words])
+
+            passes = W_OF_ROUND.get(j, [])
+            w_grouped = {}
+
+            def regroup_w(i):
+                if i < len(passes):
+                    w_grouped[i] = regroup(w_raw_of[passes[i]][:], HEAD_SHARE if j < HALF else SHARE)
+
+            def quantise_w(i):
+                if i < len(passes):
+                    quantise(w_grouped[i], w_codes[:, passes[i], :], w_scales[:, passes[i], :])
+
+            if j < HALF:
+                quantise_blocks(0, 2)
+                regroup_w(0)
+                quantise_blocks(2, 4)
+                quantise_w(0)
+                regroup_w(1)
+                quantise_blocks(4, 5)
+                quantise_w(1)
+            else:
+                regroup_w(0)
+                quantise_blocks(0, 2)
+                quantise_w(0)
+                regroup_w(1)
+                quantise_blocks(2, 4)
+                quantise_w(1)
             return x_codes, x_scales
 
         z_acc = {}
 
-        def multiply_round(j, x_codes, x_scales):
-            graph, first_pass, last_pass, blocks = plan_of_round(j)
-            for blk, (t, pair) in enumerate(blocks):
-                for g2 in range(2):
-                    g = 2 * pair + g2
-                    if g == first_pass:
-                        z_acc[t] = acc.tile([P, H], F32, tag="acc", name="z_acc")
-                    nodes = slice((blk * 2 + g2) * P, (blk * 2 + g2 + 1) * P)
-                    nc.tensor.matmul_mx(
-                        out=z_acc[t][:],
-                        lhsT=x_codes[:, nodes].bitcast(FP8X4),
-                        lhsT_scale=x_scales[:, nodes],
-                        rhs=w_codes[:, g, :].bitcast(FP8X4),
-                        rhs_scale=w_scales[:, g, :],
-                        start=(g == first_pass),
-                        stop=(g == last_pass),
-                    )
-                if 2 * pair + 1 != last_pass:
+        def multiply(out_ap, x, at, g, cols, start, stop):
+            x_codes, x_scales = x
+            nodes = slice(at * P, (at + 1) * P)
+            nc.tensor.matmul_mx(
+                out=out_ap,
+                lhsT=x_codes[:, nodes].bitcast(FP8X4),
+                lhsT_scale=x_scales[:, nodes],
+                rhs=w_codes[:, g, cols].bitcast(FP8X4),
+                rhs_scale=w_scales[:, g, cols],
+                start=start,
+                stop=stop,
+            )
+
+        def multiply_round(j, x, steps):
+            for blk, g2 in steps:
+                b, t, pair = ROUNDS[j][blk]
+                g = 2 * pair + g2
+                split = b == 0
+                first = PASSES // 2 if split and g >= PASSES // 2 else 0
+                last = PASSES // 2 - 1 if split and g < PASSES // 2 else PASSES - 1
+                if g == first:
+                    z_acc[b, t] = bank(ACC_BANK[b, t, 1 if first else 0], [P, H])
+                multiply(z_acc[b, t][:], x, 2 * blk + g2, g, slice(0, H), g == first, g == last)
+                if g != last:
                     continue
-                if last_pass != PASSES - 1:
+                if last != PASSES - 1:
                     if t % 2 == 0:
-                        nc.scalar.copy(out=z_part[t][:], in_=z_acc[t][:])
+                        nc.scalar.copy(out=z_part[t][:], in_=z_acc[b, t][:])
                     else:
-                        nc.vector.tensor_copy(out=z_part[t][:], in_=z_acc[t][:])
-                    continue
-                if first_pass == 0:
-                    nc.scalar.copy(out=z_flat[graph][:, t, :], in_=z_acc[t][:])
+                        nc.vector.tensor_copy(out=z_part[t][:], in_=z_acc[b, t][:])
+                elif first == 0:
+                    if t % 2 == 0:
+                        nc.scalar.copy(out=z_flat[b][:, t, :], in_=z_acc[b, t][:])
+                    else:
+                        nc.vector.tensor_copy(out=z_flat[b][:, t, :], in_=z_acc[b, t][:])
                 else:
                     nc.vector.tensor_tensor(
-                        out=z_flat[graph][:, t, :], in0=z_acc[t][:], in1=z_part[t][:], op=ALU.add
+                        out=z_flat[b][:, t, :], in0=z_acc[b, t][:], in1=z_part[t][:], op=ALU.add
                     )
-                if t == TILES - 1:
-                    quantise(regroup(z_flat[graph], 0), z_codes[graph][:], z_scales[graph][:])
 
-        def quarter_of_a(b, t):
-            nc.vector.scalar_tensor_tensor(
-                out=a_flat[b][:, t, :].rearrange("p (q s) -> p q s", s=TILES),
-                in0=adj_rows[b][:, t, :].rearrange("p (q s) -> p q s", s=TILES),
-                scalar=d_cols[b][:, t : t + 1],
-                in1=d_all[b][:].rearrange("p s q -> p q s"),
-                op0=ALU.mult,
-                op1=ALU.mult,
+        def multiply_second(o_acc, b, it, cols):
+            rows = slice(it * P, (it + 1) * P)
+            nc.tensor.matmul_mx(
+                out=o_acc,
+                lhsT=a_codes[b][:, rows].bitcast(FP8X4),
+                lhsT_scale=a_scales[b][:, rows],
+                rhs=z_codes[b][:, cols].bitcast(FP8X4),
+                rhs_scale=z_scales[b][:, cols],
+                start=True,
+                stop=True,
             )
-            if t == TILES - 1:
-                quantise(regroup(a_flat[b], 0), a_codes[b][:], a_scales[b][:])
 
-        def multiply_second(b):
-            sums = []
-            for it in range(TILES):
-                rows = slice(it * P, (it + 1) * P)
-                o_acc = acc.tile([P, H], F32, tag="acc")
-                nc.tensor.matmul_mx(
-                    out=o_acc[:],
-                    lhsT=a_codes[b][:, rows].bitcast(FP8X4),
-                    lhsT_scale=a_scales[b][:, rows],
-                    rhs=z_codes[b][:].bitcast(FP8X4),
-                    rhs_scale=z_scales[b][:],
-                    start=True,
-                    stop=True,
-                )
-                biased = outp.tile([P, H], F32)
+        def second_of_graph_1(its):
+            sums = {}
+            for it in its:
+                o_acc = bank(OUT_BANK_1[it], [P, H])
+                multiply_second(o_acc[:], 1, it, slice(0, H))
+                biased = outp.tile([P, H], F32, name="biased")
                 nc.vector.tensor_tensor(out=biased[:], in0=o_acc[:], in1=bias_all[:], op=ALU.add)
-                sums.append(biased)
+                sums[it] = biased
             return sums
 
         def relu_and_store(b, sums):
-            for it in range(TILES):
-                result = outp.tile([P, H], F32)
-                nc.scalar.activation(out=result[:], in_=sums[it][:], func=ACT.Relu)
+            for it, biased in sums.items():
+                result = outp.tile([P, H], F32, name="result")
+                nc.scalar.activation(out=result[:], in_=biased[:], func=ACT.Relu)
                 nc.sync.dma_start(out=out[b, it * P : (it + 1) * P, :], in_=result[:])
 
-        def prepare_round(j):
-            x_grouped = transpose_round(j)
-            w_grouped = [regroup(w_raw_of[g], SCALAR_COLS) for g in w_passes_of_round(j)]
-            codes_and_scales = quantise_round(x_grouped)
-            for g, grouped in zip(w_passes_of_round(j), w_grouped):
-                quantise(grouped, w_codes[:, g, :], w_scales[:, g, :])
-            if HALF <= j < HALF + B * TILES:
-                quarter_of_a(*divmod(j - HALF, TILES))
-            return codes_and_scales
+        out_banks = list(OUT_BANK_0)
+
+        def second_of_columns(part):
+            cols = slice(*part)
+            width = part[1] - part[0]
+            per = H // width
+            for first in range(0, TILES, per):
+                o_acc = bank(out_banks.pop(0), [P, per, width])
+                for i in range(per):
+                    multiply_second(o_acc[:, i, :], 0, first + i, cols)
+                biased = outp.tile([P, per, width], F32, name="biased")
+                nc.vector.tensor_tensor(
+                    out=biased[:], in0=o_acc[:],
+                    in1=bias_all[:, cols].unsqueeze(1).to_broadcast([P, per, width]), op=ALU.add,
+                )
+                result = outp.tile([P, per, width], F32, name="result")
+                nc.scalar.activation(out=result[:], in_=biased[:], func=ACT.Relu)
+                nc.sync.dma_start(
+                    out=out[0, first * P : (first + per) * P, cols].rearrange("(i p) c -> p i c", i=per),
+                    in_=result[:],
+                )
+
+        z_last = []
+
+        def last_tile_first_half(x):
+            for i, part in enumerate(LAST_PARTS):
+                z_last.append(bank(LAST_BANK[i], [P, part[1] - part[0]]))
+                for g in range(PASSES // 2):
+                    multiply(z_last[i][:], x, g, g, slice(*part), g == 0, False)
+
+        def last_tile_second_half(x):
+            for i, part in enumerate(LAST_PARTS):
+                for g in range(PASSES // 2, PASSES):
+                    multiply(z_last[i][:], x, g - PASSES // 2, g, slice(*part), False, g == PASSES - 1)
+            grouped = {}
+            n = len(LAST_PARTS)
+
+            def quantise_part(i):
+                cols = slice(*LAST_PARTS[i])
+                quantise(grouped[i], z_codes[0][:, cols], z_scales[0][:, cols])
+
+            for i, part in enumerate(LAST_PARTS):
+                cols = slice(*part)
+                nc.scalar.copy(out=z_flat[0][:, TILES - 1, cols], in_=z_last[i][:])
+                grouped[i] = regroup(z_flat[0][:, :, cols], LAST_SHARE)
+                if i > 0:
+                    quantise_part(i - 1)
+            quantise_part(n - 1)
+            for part in LAST_PARTS:
+                second_of_columns(part)
 
         ready = prepare_round(0)
-        d_cols = []
-        for b in range(B):
-            d_t = tr.tile([P, TILES, P], F32, tag="tr")
-            for t in range(TILES):
-                nc.tensor.transpose(d_t[:, t, :], d_all[b][:, t, :], ident[:])
-            d_col = keep.tile([P, TILES], F32, name="d_col%d" % b)
-            nc.vector.tensor_copy(out=d_col[:], in_=d_t[:, :, 0])
-            d_cols.append(d_col)
-        for j in range(ROUNDS):
-            following = prepare_round(j + 1) if j + 1 < ROUNDS else None
-            if j == LAST_OF_GRAPH_1 + SECOND_STAGE_LAG + 1:
-                relu_and_store(1, sums_of_graph_1)
-            multiply_round(j, *ready)
+        sums = {}
+        for j in range(LAST + 1):
+            n = len(ROUNDS[j])
+            if j < HALF:
+                steps = [(blk, g2) for g2 in range(2) for blk in range(n)]
+            else:
+                steps = [(blk, g2) for blk in range(n) for g2 in range(2)]
+            early = EARLY.get(j, 0)
+            multiply_round(j, ready, steps[:early])
+            following = prepare_round(j + 1) if j < LAST else None
+            relu_and_store(1, sums)
+            sums = {}
+            if j < LAST - 1:
+                multiply_round(j, ready, steps[early:])
+            elif j == LAST - 1:
+                last_tile_first_half(ready)
+            else:
+                last_tile_second_half(ready)
             ready = following
-            if j == LAST_OF_GRAPH_1 + SECOND_STAGE_LAG:
-                sums_of_graph_1 = multiply_second(1)
-        relu_and_store(0, multiply_second(0))
+            if j == C_AT:
+                column_sums()
+            if j == C_AT + 1:
+                d_columns()
+            for b, step in A_AT.get(j, []):
+                if step < TILES:
+                    products_of_d(b, step)
+                elif step == TILES:
+                    mask_a(b)
+                else:
+                    quantise_a(b)
+            if j == HALF + 2 + HALF:
+                quantise(regroup(z_flat[1][:], 0), z_codes[1][:], z_scales[1][:])
+            if j in SECOND_AFTER:
+                sums = second_of_graph_1(SECOND_AFTER[j])

@@ -37,13 +37,16 @@ LOADS = ["x1", "w2", "w3", "x2", "w4", "w5", "x3", "w6", "w7", "x4", "x5", "w8",
 ACC_BANK = {(0, 0, 0): 0, (0, 1, 0): 1, (0, 2, 0): 2, (1, 0, 0): 3, (1, 1, 0): 4, (1, 2, 0): 0, (1, 3, 0): 1,
             (0, 0, 1): 3, (0, 1, 1): 4, (0, 2, 1): 3}
 OUT_BANK_1 = [1, 0, 1, 0]
-LAST_BANK = [4, 3]
-OUT_BANK_0 = [1, 0, 2, 5, 6, 7]
+DD_ON_S = [0]
+Z1_SHARE = 128
+Z1_ON_S = [0, 1, 2, 3]
+LAST_BANK = [4, 3, 2]
+OUT_BANK_0 = [[1, 0], [5], [6]]
 C_AT = 7
 A_AT = {8: [(1, 0), (1, 1), (1, 2), (1, 3)], 9: [(1, 4)], 10: [(1, 5)], 11: [(0, 0), (0, 1), (0, 2), (0, 3)], 12: [(0, 4)], 13: [(0, 5)]}
-SECOND_AFTER = {12: [0, 1], 13: [2, 3]}
-LAST_PARTS = [(0, 256), (256, 512)]
-LAST_SHARE = 64
+SECOND_AFTER = {11: [0, 1], 12: [2, 3]}
+LAST_PARTS = [(0, 256), (256, 384), (384, 512)]
+LAST_SHARE = [96, 32, 32]
 HEAD_SHARE = 128
 SHARE = 128
 EARLY = {3: 5}
@@ -63,7 +66,7 @@ def tile_perception_pa_k_kernel(tc, batch_graph, adj, W1, b1, out):
         xq_pool = ctx.enter_context(tc.tile_pool(name="xq", bufs=3))
         wraw_pool = ctx.enter_context(tc.tile_pool(name="wraw", bufs=4))
         grp_pool = ctx.enter_context(tc.tile_pool(name="grp", bufs=3))
-        outp = ctx.enter_context(tc.tile_pool(name="outp", bufs=4))
+        outp = ctx.enter_context(tc.tile_pool(name="outp", bufs=6))
         psum = ctx.enter_context(tc.psum_pool(name="psum", bufs=1))
 
         def bank(i, shape):
@@ -96,7 +99,8 @@ def tile_perception_pa_k_kernel(tc, batch_graph, adj, W1, b1, out):
 
         def load_w(g):
             w_raw = wraw_pool.tile([P, PACK, H], BF16)
-            nc.sync.dma_start(out=w_raw[:].rearrange("q (u e) c -> q u e c", u=2), in_=w_view[g])
+            for u in range(2):
+                nc.sync.dma_start(out=w_raw[:, 2 * u : 2 * u + 2, :], in_=w_view[g][:, u])
             w_raw_of[g] = w_raw
 
         def load_x_blocks(j, first, last):
@@ -201,9 +205,12 @@ def tile_perception_pa_k_kernel(tc, batch_graph, adj, W1, b1, out):
         a_grouped = {}
 
         def products_of_d(b, t):
-            nc.vector.tensor_scalar_mul(
-                out=dd[b][:, t, :], in0=d_all[b][:], scalar1=d_cols[b][:, t : t + 1]
-            )
+            if b in DD_ON_S:
+                nc.scalar.mul(out=dd[b][:, t, :], in_=d_all[b][:], mul=d_cols[b][:, t : t + 1])
+            else:
+                nc.vector.tensor_scalar_mul(
+                    out=dd[b][:, t, :], in0=d_all[b][:], scalar1=d_cols[b][:, t : t + 1]
+                )
 
         def mask_a(b):
             grouped = grp_pool.tile([P, N * PACK], BF16, name="grouped", align_bytes=64)
@@ -218,7 +225,7 @@ def tile_perception_pa_k_kernel(tc, batch_graph, adj, W1, b1, out):
         def quantise_a(b):
             quantise(a_grouped[b], a_codes[b][:], a_scales[b][:])
 
-        def prepare_round(j):
+        def prepare_round(j, between):
             blocks = ROUNDS[j]
             x_grouped = xgrp_pool.tile([P, len(HEAD) * PAIR_K], BF16, align_bytes=64)
             x_codes = xq_pool.tile([P, len(HEAD) * PAIR_K // PACK], U32, align_bytes=64)
@@ -228,13 +235,20 @@ def tile_perception_pa_k_kernel(tc, batch_graph, adj, W1, b1, out):
                 "p (blk g r u) -> p blk g r u", g=2, r=P, u=2
             )
             banks = tr_banks(j)
-            for blk in range(len(blocks)):
+
+            def transpose(blk):
                 x_t = bank(banks[(j + blk) % len(banks)], [P, 2, 2, P])
                 for g in range(2):
                     for u in range(2):
                         first = ((blk * 2 + g) * 2 + u) * P
                         nc.tensor.transpose(x_t[:, g, u, :], x_words[:, first : first + P], ident[:])
                 nc.scalar.copy(out=grouped_words[:, blk], in_=x_t[:].rearrange("p g u r -> p g r u"))
+
+            for blk in range(min(3, len(blocks)) if j <= HALF else len(blocks)):
+                transpose(blk)
+            between()
+            for blk in range(3, len(blocks) if j <= HALF else 0):
+                transpose(blk)
 
             def quantise_blocks(first, last):
                 values = slice(first * PAIR_K, last * PAIR_K)
@@ -302,7 +316,7 @@ def tile_perception_pa_k_kernel(tc, batch_graph, adj, W1, b1, out):
                     else:
                         nc.vector.tensor_copy(out=z_part[t][:], in_=z_acc[b, t][:])
                 elif first == 0:
-                    if t % 2 == 0:
+                    if t in Z1_ON_S:
                         nc.scalar.copy(out=z_flat[b][:, t, :], in_=z_acc[b, t][:])
                     else:
                         nc.vector.tensor_copy(out=z_flat[b][:, t, :], in_=z_acc[b, t][:])
@@ -339,58 +353,56 @@ def tile_perception_pa_k_kernel(tc, batch_graph, adj, W1, b1, out):
                 nc.scalar.activation(out=result[:], in_=biased[:], func=ACT.Relu)
                 nc.sync.dma_start(out=out[b, it * P : (it + 1) * P, :], in_=result[:])
 
-        out_banks = list(OUT_BANK_0)
+        z_last = {}
+        z_grouped = {}
+        o_last = {}
 
-        def second_of_columns(part):
+        def z_of_part(i, xs, halves):
+            part = LAST_PARTS[i]
+            if 0 in halves:
+                z_last[i] = bank(LAST_BANK[i], [P, part[1] - part[0]])
+            for half in halves:
+                for step in range(PASSES // 2):
+                    g = half * PASSES // 2 + step
+                    multiply(z_last[i][:], xs[half], step, g, slice(*part), g == 0, g == PASSES - 1)
+
+        def regroup_part(i):
+            cols = slice(*LAST_PARTS[i])
+            nc.scalar.copy(out=z_flat[0][:, TILES - 1, cols], in_=z_last[i][:])
+            z_grouped[i] = regroup(z_flat[0][:, :, cols], LAST_SHARE[i])
+
+        def quantise_part(i):
+            cols = slice(*LAST_PARTS[i])
+            quantise(z_grouped[i], z_codes[0][:, cols], z_scales[0][:, cols])
+
+        def second_of_part(i):
+            part = LAST_PARTS[i]
+            per = H // (part[1] - part[0])
+            o_last[i] = []
+            for n, first in enumerate(range(0, TILES, per)):
+                o_acc = bank(OUT_BANK_0[i][n], [P, per, part[1] - part[0]])
+                for it in range(per):
+                    multiply_second(o_acc[:, it, :], 0, first + it, slice(*part))
+                o_last[i].append(o_acc)
+
+        def finish_part(i, n, first, count):
+            part = LAST_PARTS[i]
             cols = slice(*part)
             width = part[1] - part[0]
-            per = H // width
-            for first in range(0, TILES, per):
-                o_acc = bank(out_banks.pop(0), [P, per, width])
-                for i in range(per):
-                    multiply_second(o_acc[:, i, :], 0, first + i, cols)
-                biased = outp.tile([P, per, width], F32, name="biased")
-                nc.vector.tensor_tensor(
-                    out=biased[:], in0=o_acc[:],
-                    in1=bias_all[:, cols].unsqueeze(1).to_broadcast([P, per, width]), op=ALU.add,
-                )
-                result = outp.tile([P, per, width], F32, name="result")
-                nc.scalar.activation(out=result[:], in_=biased[:], func=ACT.Relu)
-                nc.sync.dma_start(
-                    out=out[0, first * P : (first + per) * P, cols].rearrange("(i p) c -> p i c", i=per),
-                    in_=result[:],
-                )
+            row = n * (H // width) + first
+            biased = outp.tile([P, H], F32, name="biased")[:, : count * width].rearrange("p (i c) -> p i c", i=count)
+            nc.vector.tensor_tensor(
+                out=biased, in0=o_last[i][n][:, first : first + count, :],
+                in1=bias_all[:, cols].unsqueeze(1).to_broadcast([P, count, width]), op=ALU.add,
+            )
+            result = outp.tile([P, H], F32, name="result")[:, : count * width].rearrange("p (i c) -> p i c", i=count)
+            nc.scalar.activation(out=result, in_=biased, func=ACT.Relu)
+            nc.sync.dma_start(
+                out=out[0, row * P : (row + count) * P, cols].rearrange("(i p) c -> p i c", i=count),
+                in_=result,
+            )
 
-        z_last = []
-
-        def last_tile_first_half(x):
-            for i, part in enumerate(LAST_PARTS):
-                z_last.append(bank(LAST_BANK[i], [P, part[1] - part[0]]))
-                for g in range(PASSES // 2):
-                    multiply(z_last[i][:], x, g, g, slice(*part), g == 0, False)
-
-        def last_tile_second_half(x):
-            for i, part in enumerate(LAST_PARTS):
-                for g in range(PASSES // 2, PASSES):
-                    multiply(z_last[i][:], x, g - PASSES // 2, g, slice(*part), False, g == PASSES - 1)
-            grouped = {}
-            n = len(LAST_PARTS)
-
-            def quantise_part(i):
-                cols = slice(*LAST_PARTS[i])
-                quantise(grouped[i], z_codes[0][:, cols], z_scales[0][:, cols])
-
-            for i, part in enumerate(LAST_PARTS):
-                cols = slice(*part)
-                nc.scalar.copy(out=z_flat[0][:, TILES - 1, cols], in_=z_last[i][:])
-                grouped[i] = regroup(z_flat[0][:, :, cols], LAST_SHARE)
-                if i > 0:
-                    quantise_part(i - 1)
-            quantise_part(n - 1)
-            for part in LAST_PARTS:
-                second_of_columns(part)
-
-        ready = prepare_round(0)
+        ready = prepare_round(0, lambda: None)
         sums = {}
         for j in range(LAST + 1):
             n = len(ROUNDS[j])
@@ -398,17 +410,36 @@ def tile_perception_pa_k_kernel(tc, batch_graph, adj, W1, b1, out):
                 steps = [(blk, g2) for g2 in range(2) for blk in range(n)]
             else:
                 steps = [(blk, g2) for blk in range(n) for g2 in range(2)]
-            early = EARLY.get(j, 0)
-            multiply_round(j, ready, steps[:early])
-            following = prepare_round(j + 1) if j < LAST else None
+            early = n if j < HALF else 0
+            following = None
+            if j < LAST:
+                following = prepare_round(j + 1, lambda: multiply_round(j, ready, steps[:early]))
             relu_and_store(1, sums)
             sums = {}
             if j < LAST - 1:
                 multiply_round(j, ready, steps[early:])
             elif j == LAST - 1:
-                last_tile_first_half(ready)
+                x_last = [ready, following]
+                z_of_part(0, x_last, [0])
+                z_of_part(1, x_last, [0])
             else:
-                last_tile_second_half(ready)
+                z_of_part(0, x_last, [1])
+                z_of_part(1, x_last, [1])
+                z_of_part(2, x_last, [0, 1])
+                regroup_part(0)
+                regroup_part(1)
+                quantise_part(0)
+                second_of_part(0)
+                quantise_part(1)
+                second_of_part(1)
+                regroup_part(2)
+                finish_part(0, 0, 0, 2)
+                quantise_part(2)
+                second_of_part(2)
+                finish_part(0, 1, 0, 2)
+                finish_part(1, 0, 0, 4)
+                finish_part(2, 0, 0, 2)
+                finish_part(2, 0, 2, 2)
             ready = following
             if j == C_AT:
                 column_sums()
@@ -422,6 +453,6 @@ def tile_perception_pa_k_kernel(tc, batch_graph, adj, W1, b1, out):
                 else:
                     quantise_a(b)
             if j == HALF + 2 + HALF:
-                quantise(regroup(z_flat[1][:], 0), z_codes[1][:], z_scales[1][:])
+                quantise(regroup(z_flat[1][:], Z1_SHARE), z_codes[1][:], z_scales[1][:])
             if j in SECOND_AFTER:
                 sums = second_of_graph_1(SECOND_AFTER[j])

@@ -110,10 +110,11 @@ def tile_perception_pa_k_kernel(tc, batch_graph, adj, W1, b1, out):
             if n > 1 and ROUNDS[j][first + 1][1] == t:
                 nc.sync.dma_start(out=dst, in_=x_views[b][:, t, pair * PAIR_K : (pair + n) * PAIR_K])
             else:
-                nc.sync.dma_start(
-                    out=dst.rearrange("p (t k) -> p t k", t=n),
-                    in_=x_views[b][:, t : t + n, pair * PAIR_K : (pair + 1) * PAIR_K],
-                )
+                for i in range(n):
+                    nc.sync.dma_start(
+                        out=dst[:, i * PAIR_K : (i + 1) * PAIR_K],
+                        in_=x_views[b][:, t + i, pair * PAIR_K : (pair + 1) * PAIR_K],
+                    )
 
         def new_x(j):
             x_raw_of[j] = xraw_pool.tile([P, len(HEAD) * PAIR_K], BF16, name="x_raw")

@@ -139,19 +139,19 @@ def tile_perception_pa_k_kernel(tc, batch_graph, adj, W1, b1, out):
                 else:
                     load_x_blocks(j, 0, 3)
 
-        w_codes = keep.tile([P, PASSES, H], U32, align_bytes=64)
-        w_scales = keep.tile([P, PASSES, H], U8, align_bytes=64)
+        w_codes = keep.tile([P, PASSES, H], U32, align_bytes=256)
+        w_scales = keep.tile([P, PASSES, H], U8, align_bytes=256)
         dd = [keep.tile([P, TILES, N], BF16, name="dd%d" % b) for b in range(B)]
         z_flat = [keep.tile([P, TILES, H], BF16, name="z_flat%d" % b) for b in range(B)]
         z_part = [keep.tile([P, H], F32, name="z_part%d" % t) for t in range(TILES - 1)]
-        a_codes = [keep.tile([P, N], U32, name="a_codes%d" % b, align_bytes=64) for b in range(B)]
-        a_scales = [keep.tile([P, N], U8, name="a_scales%d" % b, align_bytes=64) for b in range(B)]
-        z_codes = [keep.tile([P, H], U32, name="z_codes%d" % b, align_bytes=64) for b in range(B)]
-        z_scales = [keep.tile([P, H], U8, name="z_scales%d" % b, align_bytes=64) for b in range(B)]
+        a_codes = [keep.tile([P, N], U32, name="a_codes%d" % b, align_bytes=256) for b in range(B)]
+        a_scales = [keep.tile([P, N], U8, name="a_scales%d" % b, align_bytes=256) for b in range(B)]
+        z_codes = [keep.tile([P, H], U32, name="z_codes%d" % b, align_bytes=256) for b in range(B)]
+        z_scales = [keep.tile([P, H], U8, name="z_scales%d" % b, align_bytes=256) for b in range(B)]
 
         def regroup(flat, scalar_cols):
             width = flat.shape[2]
-            grouped = grp_pool.tile([P, H * PACK], BF16, name="grouped", align_bytes=64)[:, : width * PACK]
+            grouped = grp_pool.tile([P, H * PACK], BF16, name="grouped", align_bytes=256)[:, : width * PACK]
             by_col = grouped.rearrange("p (c t) -> p c t", t=PACK)
             split = width - scalar_cols
             nc.vector.tensor_copy(
@@ -214,7 +214,7 @@ def tile_perception_pa_k_kernel(tc, batch_graph, adj, W1, b1, out):
                 )
 
         def mask_a(b):
-            grouped = grp_pool.tile([P, N * PACK], BF16, name="grouped", align_bytes=64)
+            grouped = grp_pool.tile([P, N * PACK], BF16, name="grouped", align_bytes=256)
             nc.vector.tensor_tensor(
                 out=grouped[:].rearrange("p (c i t) -> p c t i", i=4, t=PACK),
                 in0=adj_rows[b][:].rearrange("p t (c i) -> p c t i", i=4),
@@ -228,9 +228,9 @@ def tile_perception_pa_k_kernel(tc, batch_graph, adj, W1, b1, out):
 
         def prepare_round(j, between):
             blocks = ROUNDS[j]
-            x_grouped = xgrp_pool.tile([P, len(HEAD) * PAIR_K], BF16, align_bytes=64)
-            x_codes = xq_pool.tile([P, len(HEAD) * PAIR_K // PACK], U32, align_bytes=64)
-            x_scales = xq_pool.tile([P, len(HEAD) * PAIR_K // PACK], U8, align_bytes=64)
+            x_grouped = xgrp_pool.tile([P, len(HEAD) * PAIR_K], BF16, align_bytes=256)
+            x_codes = xq_pool.tile([P, len(HEAD) * PAIR_K // PACK], U32, align_bytes=256)
+            x_scales = xq_pool.tile([P, len(HEAD) * PAIR_K // PACK], U8, align_bytes=256)
             x_words = x_raw_of[j][:].bitcast(F32)
             grouped_words = x_grouped[:].bitcast(F32).rearrange(
                 "p (blk g r u) -> p blk g r u", g=2, r=P, u=2

@@ -40,8 +40,8 @@ OUT_BANK_1 = [1, 0, 1, 0]
 DD_ON_S = [0]
 Z1_SHARE = 128
 Z1_ON_S = [0, 1, 2, 3]
-LAST_BANK = [4, 3, 2]
-OUT_BANK_0 = [[1, 0], [5], [6]]
+LAST_BANK = [4, 3, 0]
+OUT_BANK_0 = [[1, 2], [5], [6]]
 C_AT = 7
 A_AT = {8: [(1, 0), (1, 1), (1, 2), (1, 3)], 9: [(1, 4)], 10: [(1, 5)], 11: [(0, 0), (0, 1), (0, 2), (0, 3)], 12: [(0, 4)], 13: [(0, 5)]}
 SECOND_AFTER = {11: [0, 1], 12: [2, 3]}
@@ -78,6 +78,8 @@ def tile_perception_pa_k_kernel(tc, batch_graph, adj, W1, b1, out):
         nc.vector.memset(ones[:], 1.0)
         bias_rows = keep.tile([P, H], BF16)
         nc.vector.memset(bias_rows[:], 0.0)
+        fill = keep.tile([P, H], BF16)
+        nc.vector.memset(fill[:], 1.0)
         floor_col = keep.tile([P, 1], F32)
         nc.vector.memset(floor_col[:], 1e-30)
         warm = keep.tile([P, 1], F32)
@@ -236,6 +238,9 @@ def tile_perception_pa_k_kernel(tc, batch_graph, adj, W1, b1, out):
                 "p (blk g r u) -> p blk g r u", g=2, r=P, u=2
             )
             banks = tr_banks(j)
+            for i in range({4: 5, 9: 2}.get(j, 0)):
+                unread = bank(banks[j % len(banks)], [P, H])
+                nc.tensor.matmul(out=unread[:], lhsT=ones[:], rhs=fill[:], start=True, stop=True)
 
             def transpose(blk):
                 x_t = bank(banks[(j + blk) % len(banks)], [P, 2, 2, P])
@@ -423,10 +428,11 @@ def tile_perception_pa_k_kernel(tc, batch_graph, adj, W1, b1, out):
                 x_last = [ready, following]
                 z_of_part(0, x_last, [0])
                 z_of_part(1, x_last, [0])
+                z_of_part(2, x_last, [0])
             else:
                 z_of_part(0, x_last, [1])
                 z_of_part(1, x_last, [1])
-                z_of_part(2, x_last, [0, 1])
+                z_of_part(2, x_last, [1])
                 regroup_part(0)
                 regroup_part(1)
                 quantise_part(0)

@@ -33,15 +33,15 @@ ROUNDS = (
 )
 LAST = len(ROUNDS) - 1
 W_OF_ROUND = {0: [0, 1], 1: [2, 3], 2: [4, 5], 3: [6, 7], 5: [8, 9], 6: [10], 7: [11, 12], 8: [13, 14], 9: [15]}
-LOADS = ["x1", "w2", "w3", "x2", "w4", "w5", "x3", "w6", "w7", "x4", "x5", "w8", "w9", "x6", "w10", "x7", "w11", "w12", "x8", "adj", "w13", "w14", "x9", "w15", "x10", "x11", "x12", "x13", "x14"]
+LOADS = ["x1","w2","w3","x2","w4","w5","x3","w6","x4","w7","x5","w8","w9","x6","w10","x7","w11","w12","adj","x8","w13","w14","x9","w15","x10","x11","x12","x13","x14"]
 ACC_BANK = {(0, 0, 0): 0, (0, 1, 0): 1, (0, 2, 0): 2, (1, 0, 0): 3, (1, 1, 0): 4, (1, 2, 0): 0, (1, 3, 0): 1,
             (0, 0, 1): 3, (0, 1, 1): 4, (0, 2, 1): 3}
 OUT_BANK_1 = [1, 0, 1, 0]
 DD_ON_S = [0]
 Z1_SHARE = 128
 Z1_ON_S = [0, 1, 2, 3]
-LAST_BANK = [4, 3, 0]
-OUT_BANK_0 = [[1, 2], [5], [6]]
+LAST_BANK = [4, 3, 7]
+OUT_BANK_0 = [[1, 0], [5], [6]]
 C_AT = 7
 A_AT = {8: [(1, 0), (1, 1), (1, 2), (1, 3)], 9: [(1, 4)], 10: [(1, 5)], 11: [(0, 0), (0, 1), (0, 2), (0, 3)], 12: [(0, 4)], 13: [(0, 5)]}
 SECOND_AFTER = {11: [0, 1], 12: [2, 3]}
@@ -78,8 +78,6 @@ def tile_perception_pa_k_kernel(tc, batch_graph, adj, W1, b1, out):
         nc.vector.memset(ones[:], 1.0)
         bias_rows = keep.tile([P, H], BF16)
         nc.vector.memset(bias_rows[:], 0.0)
-        fill = keep.tile([P, H], BF16)
-        nc.vector.memset(fill[:], 1.0)
         floor_col = keep.tile([P, 1], F32)
         nc.vector.memset(floor_col[:], 1e-30)
         warm = keep.tile([P, 1], F32)
@@ -92,7 +90,6 @@ def tile_perception_pa_k_kernel(tc, batch_graph, adj, W1, b1, out):
                 adj_b = keep.tile([P, TILES, N], BF16, name="adj_rows%d" % b)
                 nc.sync.dma_start(out=adj_b[:], in_=adj[b].rearrange("(p t) i -> p t i", t=TILES))
                 adj_rows.append(adj_b)
-            nc.sync.dma_start(out=bias_rows[0:1, :], in_=b1.unsqueeze(0))
 
         w_view = W1.rearrange("(g u q e) c -> g q u e c", u=2, q=P, e=2)
         x_views = [batch_graph[b].rearrange("(p t) k -> p t k", t=TILES) for b in range(B)]
@@ -127,6 +124,7 @@ def tile_perception_pa_k_kernel(tc, batch_graph, adj, W1, b1, out):
         load_w(0)
         load_x_blocks(0, 3, 4)
         load_w(1)
+        nc.sync.dma_start(out=bias_rows[0:1, :], in_=b1.unsqueeze(0))
         for what in LOADS:
             if what == "adj":
                 load_adj_and_bias()
@@ -170,40 +168,43 @@ def tile_perception_pa_k_kernel(tc, batch_graph, adj, W1, b1, out):
         def quantise(grouped, codes, scales):
             nc.vector.quantize_mx(out=codes.bitcast(FP8X4), scales=scales, in_=grouped)
 
-        d_all = []
-        d_cols = []
+        d_all = {}
+        d_cols = {}
         bias_all = keep.tile([P, H], F32)
 
-        def column_sums():
-            for b in range(B):
-                c_sum = bank(tr_banks(LAST)[b], [P, N])
-                for t in range(TILES):
-                    nc.tensor.matmul(
-                        out=c_sum[:], lhsT=ones[:], rhs=adj_rows[b][:, t, :],
-                        start=(t == 0), stop=(t == TILES - 1),
-                    )
-                d_b = keep.tile([P, N], F32, name="d_all%d" % b)
-                nc.scalar.activation(
-                    out=d_b[:], in_=c_sum[:], func=ACT.Abs_reciprocal_sqrt, bias=floor_col[:]
-                )
-                d_all.append(d_b)
-            bias_sum = bank(tr_banks(LAST)[2], [P, H])
-            nc.tensor.matmul(out=bias_sum[:], lhsT=ones[:], rhs=bias_rows[:], start=True, stop=True)
-            nc.scalar.copy(out=bias_all[:], in_=bias_sum[:])
+        adj_sums = {}
 
-        def d_columns():
-            for b in range(B):
-                d_t = bank(tr_banks(LAST)[b], [P, TILES, P])
-                for t in range(TILES):
-                    nc.tensor.transpose(d_t[:, t, :], d_all[b][:, t::TILES], ident[:])
-                d_raw = keep.tile([P, TILES], F32, name="d_raw%d" % b)
-                nc.vector.tensor_copy(out=d_raw[:], in_=d_t[:, :, 0])
-                d_col = keep.tile([P, TILES], F32, name="d_col%d" % b)
-                nc.vector.scalar_tensor_tensor(
-                    out=d_col[:], in0=d_raw[:], scalar=1e14, in1=d_raw[:],
-                    op0=ALU.is_lt, op1=ALU.mult,
-                )
-                d_cols.append(d_col)
+        def add_rows_of_adj(b):
+            two = grp_pool.tile([P, H * PACK], BF16, name="grouped", align_bytes=256)
+            two_rows = two[:, : 2 * N].rearrange("p (t i) -> p t i", t=2)
+            nc.vector.tensor_tensor(
+                out=two_rows, in0=adj_rows[b][:, 0:2, :], in1=adj_rows[b][:, 2:4, :], op=ALU.add
+            )
+            total = keep.tile([P, N], BF16, name="adj_sums%d" % b)
+            nc.vector.tensor_tensor(out=total[:], in0=two_rows[:, 0, :], in1=two_rows[:, 1, :], op=ALU.add)
+            adj_sums[b] = total
+
+        def column_sums(b, j):
+            c_sum = bank(tr_banks(LAST)[j % 4], [P, N])
+            nc.tensor.matmul(out=c_sum[:], lhsT=ones[:], rhs=adj_sums[b][:], start=True, stop=True)
+            d_b = keep.tile([P, N], F32, name="d_all%d" % b)
+            nc.scalar.activation(
+                out=d_b[:], in_=c_sum[:], func=ACT.Abs_reciprocal_sqrt, bias=floor_col[:]
+            )
+            d_all[b] = d_b
+
+        def d_columns(b, j):
+            d_t = bank(tr_banks(LAST)[(j + 1) % 4], [P, TILES, P])
+            for t in range(TILES):
+                nc.tensor.transpose(d_t[:, t, :], d_all[b][:, t::TILES], ident[:])
+            d_raw = keep.tile([P, TILES], F32, name="d_raw%d" % b)
+            nc.vector.tensor_copy(out=d_raw[:], in_=d_t[:, :, 0])
+            d_col = keep.tile([P, TILES], F32, name="d_col%d" % b)
+            nc.vector.scalar_tensor_tensor(
+                out=d_col[:], in0=d_raw[:], scalar=1e14, in1=d_raw[:],
+                op0=ALU.is_lt, op1=ALU.mult,
+            )
+            d_cols[b] = d_col
 
         a_grouped = {}
 
@@ -238,9 +239,6 @@ def tile_perception_pa_k_kernel(tc, batch_graph, adj, W1, b1, out):
                 "p (blk g r u) -> p blk g r u", g=2, r=P, u=2
             )
             banks = tr_banks(j)
-            for i in range({4: 5, 9: 2}.get(j, 0)):
-                unread = bank(banks[j % len(banks)], [P, H])
-                nc.tensor.matmul(out=unread[:], lhsT=ones[:], rhs=fill[:], start=True, stop=True)
 
             def transpose(blk):
                 x_t = bank(banks[(j + blk) % len(banks)], [P, 2, 2, P])
@@ -409,6 +407,9 @@ def tile_perception_pa_k_kernel(tc, batch_graph, adj, W1, b1, out):
             )
 
         ready = prepare_round(0, lambda: None)
+        bias_sum = bank(4, [P, H])
+        nc.tensor.matmul(out=bias_sum[:], lhsT=ones[:], rhs=bias_rows[:], start=True, stop=True)
+        nc.scalar.copy(out=bias_all[:], in_=bias_sum[:])
         sums = {}
         for j in range(LAST + 1):
             n = len(ROUNDS[j])
@@ -448,10 +449,15 @@ def tile_perception_pa_k_kernel(tc, batch_graph, adj, W1, b1, out):
                 finish_part(2, 0, 0, 2)
                 finish_part(2, 0, 2, 2)
             ready = following
-            if j == C_AT:
-                column_sums()
-            if j == C_AT + 1:
-                d_columns()
+            if j == C_AT - 1:
+                add_rows_of_adj(1)
+                add_rows_of_adj(0)
+            for b in range(B):
+                if j == C_AT + 1 + (1 - b):
+                    d_columns(b, j)
+            for b in range(B):
+                if j == C_AT + (1 - b):
+                    column_sums(b, j)
             for b, step in A_AT.get(j, []):
                 if step < TILES:
                     products_of_d(b, step)

from contextlib import ExitStack

import concourse.mybir as mybir
from concourse.masks import make_identity

F32 = mybir.dt.float32
BF16 = mybir.dt.bfloat16
U32 = mybir.dt.uint32
U8 = mybir.dt.uint8
FP8X4 = mybir.dt.float8_e4m3fn_x4
ALU = mybir.AluOpType
ACT = mybir.ActivationFunctionType

B, N, D, H = 2, 512, 8192, 512
FLOPS = 2 * B * N * D * H + 2 * B * N * N * H

P = 128
PACK = 4
K_PASS = P * PACK
PASSES = D // K_PASS
TILES = N // P
PAIR_K = 2 * K_PASS
PAIRS = PASSES // 2
HALF = PAIRS // 2

HEAD = [(0, 0), (0, 1), (0, 2), (1, 0), (1, 1)]
ROUNDS = (
    [[(b, t, pair) for b, t in HEAD] for pair in range(HALF)]
    + [[(1, t, pair) for pair in range(HALF)] for t in (2, 3)]
    + [[(1, t, pair) for t in range(TILES)] for pair in range(HALF, PAIRS)]
    + [[(0, t, pair) for pair in range(HALF, PAIRS)] for t in range(3)]
    + [[(0, 3, pair) for pair in range(HALF)], [(0, 3, pair) for pair in range(HALF, PAIRS)]]
)
LAST = len(ROUNDS) - 1
W_OF_ROUND = {0: [0, 1], 1: [2, 3], 2: [4, 5], 3: [6, 7], 5: [8, 9], 6: [10], 7: [11, 12], 8: [13, 14], 9: [15]}
LOADS = ["x1","w2","w3","x2","w4","w5","x3","w6","x4","w7","x5","w8","w9","x6","w10","x7","w11","w12","adj","x8","w13","w14","x9","w15","x10","x11","x12","x13","x14"]
ACC_BANK = {(0, 0, 0): 0, (0, 1, 0): 1, (0, 2, 0): 2, (1, 0, 0): 3, (1, 1, 0): 4, (1, 2, 0): 0, (1, 3, 0): 1,
            (0, 0, 1): 3, (0, 1, 1): 4, (0, 2, 1): 3}
OUT_BANK_1 = [1, 0, 1, 0]
DD_ON_S = [0]
Z1_SHARE = 128
Z1_ON_S = [0, 1, 2, 3]
LAST_BANK = [4, 3, 7]
OUT_BANK_0 = [[1, 0], [5], [6]]
C_AT = 7
A_AT = {8: [(1, 0), (1, 1), (1, 2), (1, 3)], 9: [(1, 4)], 10: [(1, 5)], 11: [(0, 0), (0, 1), (0, 2), (0, 3)], 12: [(0, 4)], 13: [(0, 5)]}
SECOND_AFTER = {11: [0, 1], 12: [2, 3]}
LAST_PARTS = [(0, 256), (256, 384), (384, 512)]
LAST_SHARE = [96, 32, 32]
HEAD_SHARE = 128
SHARE = 128
EARLY = {3: 5}


def tr_banks(j):
    return [5, 6, 7] if j <= HALF else [2, 5, 6, 7]


def tile_perception_pa_k_kernel(tc, batch_graph, adj, W1, b1, out):
    nc = tc.nc
    with ExitStack() as ctx:
        ctx.enter_context(tc.manual_schedule())
        keep = ctx.enter_context(tc.tile_pool(name="keep", bufs=1))
        xraw_pool = ctx.enter_context(tc.tile_pool(name="xraw", bufs=4))
        xgrp_pool = ctx.enter_context(tc.tile_pool(name="xgrp", bufs=2))
        xq_pool = ctx.enter_context(tc.tile_pool(name="xq", bufs=3))
        wraw_pool = ctx.enter_context(tc.tile_pool(name="wraw", bufs=4))
        grp_pool = ctx.enter_context(tc.tile_pool(name="grp", bufs=3))
        outp = ctx.enter_context(tc.tile_pool(name="outp", bufs=6))
        psum = ctx.enter_context(tc.psum_pool(name="psum", bufs=1))

        def bank(i, shape):
            return psum.tile(shape, F32, tag="bank%d" % i, name="bank")

        ident = keep.tile([P, P], F32)
        make_identity(nc, ident[:])
        ones = keep.tile([P, P], BF16)
        nc.vector.memset(ones[:], 1.0)
        bias_rows = keep.tile([P, H], BF16)
        nc.vector.memset(bias_rows[:], 0.0)
        floor_col = keep.tile([P, 1], F32)
        nc.vector.memset(floor_col[:], 1e-30)
        warm = keep.tile([P, 1], F32)
        nc.scalar.activation(out=warm[:], in_=ones[:, 0:1], func=ACT.Abs_reciprocal_sqrt)

        adj_rows = []

        def load_adj_and_bias():
            for b in range(B):
                adj_b = keep.tile([P, TILES, N], BF16, name="adj_rows%d" % b)
                nc.sync.dma_start(out=adj_b[:], in_=adj[b].rearrange("(p t) i -> p t i", t=TILES))
                adj_rows.append(adj_b)

        w_view = W1.rearrange("(g u q e) c -> g q u e c", u=2, q=P, e=2)
        x_views = [batch_graph[b].rearrange("(p t) k -> p t k", t=TILES) for b in range(B)]
        x_raw_of = {}
        w_raw_of = {}

        def load_w(g):
            w_raw = wraw_pool.tile([P, PACK, H], BF16)
            for u in range(2):
                nc.sync.dma_start(out=w_raw[:, 2 * u : 2 * u + 2, :], in_=w_view[g][:, u])
            w_raw_of[g] = w_raw

        def load_x_blocks(j, first, last):
            b, t, pair = ROUNDS[j][first]
            n = last - first + 1
            dst = x_raw_of[j][:, first * PAIR_K : (last + 1) * PAIR_K]
            if n > 1 and ROUNDS[j][first + 1][1] == t:
                nc.sync.dma_start(out=dst, in_=x_views[b][:, t, pair * PAIR_K : (pair + n) * PAIR_K])
            else:
                for i in range(n):
                    nc.sync.dma_start(
                        out=dst[:, i * PAIR_K : (i + 1) * PAIR_K],
                        in_=x_views[b][:, t + i, pair * PAIR_K : (pair + 1) * PAIR_K],
                    )

        def new_x(j):
            x_raw_of[j] = xraw_pool.tile([P, len(HEAD) * PAIR_K], BF16, name="x_raw")

        new_x(0)
        load_x_blocks(0, 0, 0)
        load_x_blocks(0, 1, 2)
        load_w(0)
        load_x_blocks(0, 3, 4)
        load_w(1)
        nc.sync.dma_start(out=bias_rows[0:1, :], in_=b1.unsqueeze(0))
        for what in LOADS:
            if what == "adj":
                load_adj_and_bias()
            elif what[0] == "w":
                load_w(int(what[1:]))
            else:
                j = int(what[1:])
                new_x(j)
                if j < HALF:
                    load_x_blocks(j, 0, 2)
                    load_x_blocks(j, 3, 4)
                else:
                    load_x_blocks(j, 0, 3)

        w_codes = keep.tile([P, PASSES, H], U32, align_bytes=256)
        w_scales = keep.tile([P, PASSES, H], U8, align_bytes=256)
        dd = [keep.tile([P, TILES, N], BF16, name="dd%d" % b) for b in range(B)]
        z_flat = [keep.tile([P, TILES, H], BF16, name="z_flat%d" % b) for b in range(B)]
        z_part = [keep.tile([P, H], F32, name="z_part%d" % t) for t in range(TILES - 1)]
        a_codes = [keep.tile([P, N], U32, name="a_codes%d" % b, align_bytes=256) for b in range(B)]
        a_scales = [keep.tile([P, N], U8, name="a_scales%d" % b, align_bytes=256) for b in range(B)]
        z_codes = [keep.tile([P, H], U32, name="z_codes%d" % b, align_bytes=256) for b in range(B)]
        z_scales = [keep.tile([P, H], U8, name="z_scales%d" % b, align_bytes=256) for b in range(B)]

        def regroup(flat, scalar_cols):
            width = flat.shape[2]
            grouped = grp_pool.tile([P, H * PACK], BF16, name="grouped", align_bytes=256)[:, : width * PACK]
            by_col = grouped.rearrange("p (c t) -> p c t", t=PACK)
            split = width - scalar_cols
            nc.vector.tensor_copy(
                out=by_col[:, :split, :].rearrange("p (c i) t -> p c t i", i=4),
                in_=flat[:, :, :split].rearrange("p t (c i) -> p c t i", i=4),
            )
            if scalar_cols > 0:
                nc.scalar.copy(
                    out=by_col[:, split:, :].rearrange("p (c i) t -> p c t i", i=4),
                    in_=flat[:, :, split:].rearrange("p t (c i) -> p c t i", i=4),
                )
            return grouped

        def quantise(grouped, codes, scales):
            nc.vector.quantize_mx(out=codes.bitcast(FP8X4), scales=scales, in_=grouped)

        d_all = {}
        d_cols = {}
        bias_all = keep.tile([P, H], F32)

        adj_sums = {}

        def add_rows_of_adj(b):
            two = grp_pool.tile([P, H * PACK], BF16, name="grouped", align_bytes=256)
            two_rows = two[:, : 2 * N].rearrange("p (t i) -> p t i", t=2)
            nc.vector.tensor_tensor(
                out=two_rows, in0=adj_rows[b][:, 0:2, :], in1=adj_rows[b][:, 2:4, :], op=ALU.add
            )
            total = keep.tile([P, N], BF16, name="adj_sums%d" % b)
            nc.vector.tensor_tensor(out=total[:], in0=two_rows[:, 0, :], in1=two_rows[:, 1, :], op=ALU.add)
            adj_sums[b] = total

        def column_sums(b, j):
            c_sum = bank(tr_banks(LAST)[j % 4], [P, N])
            nc.tensor.matmul(out=c_sum[:], lhsT=ones[:], rhs=adj_sums[b][:], start=True, stop=True)
            d_b = keep.tile([P, N], F32, name="d_all%d" % b)
            nc.scalar.activation(
                out=d_b[:], in_=c_sum[:], func=ACT.Abs_reciprocal_sqrt, bias=floor_col[:]
            )
            d_all[b] = d_b

        def d_columns(b, j):
            d_t = bank(tr_banks(LAST)[(j + 1) % 4], [P, TILES, P])
            for t in range(TILES):
                nc.tensor.transpose(d_t[:, t, :], d_all[b][:, t::TILES], ident[:])
            d_raw = keep.tile([P, TILES], F32, name="d_raw%d" % b)
            nc.vector.tensor_copy(out=d_raw[:], in_=d_t[:, :, 0])
            d_col = keep.tile([P, TILES], F32, name="d_col%d" % b)
            nc.vector.scalar_tensor_tensor(
                out=d_col[:], in0=d_raw[:], scalar=1e14, in1=d_raw[:],
                op0=ALU.is_lt, op1=ALU.mult,
            )
            d_cols[b] = d_col

        a_grouped = {}

        def products_of_d(b, t):
            if b in DD_ON_S:
                nc.scalar.mul(out=dd[b][:, t, :], in_=d_all[b][:], mul=d_cols[b][:, t : t + 1])
            else:
                nc.vector.tensor_scalar_mul(
                    out=dd[b][:, t, :], in0=d_all[b][:], scalar1=d_cols[b][:, t : t + 1]
                )

        def mask_a(b):
            grouped = grp_pool.tile([P, N * PACK], BF16, name="grouped", align_bytes=256)
            nc.vector.tensor_tensor(
                out=grouped[:].rearrange("p (c i t) -> p c t i", i=4, t=PACK),
                in0=adj_rows[b][:].rearrange("p t (c i) -> p c t i", i=4),
                in1=dd[b][:].rearrange("p t (c i) -> p c t i", i=4),
                op=ALU.mult,
            )
            a_grouped[b] = grouped[:]

        def quantise_a(b):
            quantise(a_grouped[b], a_codes[b][:], a_scales[b][:])

        def prepare_round(j, between):
            blocks = ROUNDS[j]
            x_grouped = xgrp_pool.tile([P, len(HEAD) * PAIR_K], BF16, align_bytes=256)
            x_codes = xq_pool.tile([P, len(HEAD) * PAIR_K // PACK], U32, align_bytes=256)
            x_scales = xq_pool.tile([P, len(HEAD) * PAIR_K // PACK], U8, align_bytes=256)
            x_words = x_raw_of[j][:].bitcast(F32)
            grouped_words = x_grouped[:].bitcast(F32).rearrange(
                "p (blk g r u) -> p blk g r u", g=2, r=P, u=2
            )
            banks = tr_banks(j)

            def transpose(blk):
                x_t = bank(banks[(j + blk) % len(banks)], [P, 2, 2, P])
                for g in range(2):
                    for u in range(2):
                        first = ((blk * 2 + g) * 2 + u) * P
                        nc.tensor.transpose(x_t[:, g, u, :], x_words[:, first : first + P], ident[:])
                nc.scalar.copy(out=grouped_words[:, blk], in_=x_t[:].rearrange("p g u r -> p g r u"))

            for blk in range(min(3, len(blocks)) if j <= HALF else len(blocks)):
                transpose(blk)
            between()
            for blk in range(3, len(blocks) if j <= HALF else 0):
                transpose(blk)

            def quantise_blocks(first, last):
                values = slice(first * PAIR_K, last * PAIR_K)
                words = slice(first * PAIR_K // PACK, last * PAIR_K // PACK)
                quantise(x_grouped[:, values], x_codes[:, words], x_scales[:, words])

            passes = W_OF_ROUND.get(j, [])
            w_grouped = {}

            def regroup_w(i):
                if i < len(passes):
                    w_grouped[i] = regroup(w_raw_of[passes[i]][:], HEAD_SHARE if j < HALF else SHARE)

            def quantise_w(i):
                if i < len(passes):
                    quantise(w_grouped[i], w_codes[:, passes[i], :], w_scales[:, passes[i], :])

            if j < HALF:
                quantise_blocks(0, 2)
                regroup_w(0)
                quantise_blocks(2, 4)
                quantise_w(0)
                regroup_w(1)
                quantise_blocks(4, 5)
                quantise_w(1)
            else:
                regroup_w(0)
                quantise_blocks(0, 2)
                quantise_w(0)
                regroup_w(1)
                quantise_blocks(2, 4)
                quantise_w(1)
            return x_codes, x_scales

        z_acc = {}

        def multiply(out_ap, x, at, g, cols, start, stop):
            x_codes, x_scales = x
            nodes = slice(at * P, (at + 1) * P)
            nc.tensor.matmul_mx(
                out=out_ap,
                lhsT=x_codes[:, nodes].bitcast(FP8X4),
                lhsT_scale=x_scales[:, nodes],
                rhs=w_codes[:, g, cols].bitcast(FP8X4),
                rhs_scale=w_scales[:, g, cols],
                start=start,
                stop=stop,
            )

        def multiply_round(j, x, steps):
            for blk, g2 in steps:
                b, t, pair = ROUNDS[j][blk]
                g = 2 * pair + g2
                split = b == 0
                first = PASSES // 2 if split and g >= PASSES // 2 else 0
                last = PASSES // 2 - 1 if split and g < PASSES // 2 else PASSES - 1
                if g == first:
                    z_acc[b, t] = bank(ACC_BANK[b, t, 1 if first else 0], [P, H])
                multiply(z_acc[b, t][:], x, 2 * blk + g2, g, slice(0, H), g == first, g == last)
                if g != last:
                    continue
                if last != PASSES - 1:
                    if t % 2 == 0:
                        nc.scalar.copy(out=z_part[t][:], in_=z_acc[b, t][:])
                    else:
                        nc.vector.tensor_copy(out=z_part[t][:], in_=z_acc[b, t][:])
                elif first == 0:
                    if t in Z1_ON_S:
                        nc.scalar.copy(out=z_flat[b][:, t, :], in_=z_acc[b, t][:])
                    else:
                        nc.vector.tensor_copy(out=z_flat[b][:, t, :], in_=z_acc[b, t][:])
                else:
                    nc.vector.tensor_tensor(
                        out=z_flat[b][:, t, :], in0=z_acc[b, t][:], in1=z_part[t][:], op=ALU.add
                    )

        def multiply_second(o_acc, b, it, cols):
            rows = slice(it * P, (it + 1) * P)
            nc.tensor.matmul_mx(
                out=o_acc,
                lhsT=a_codes[b][:, rows].bitcast(FP8X4),
                lhsT_scale=a_scales[b][:, rows],
                rhs=z_codes[b][:, cols].bitcast(FP8X4),
                rhs_scale=z_scales[b][:, cols],
                start=True,
                stop=True,
            )

        def second_of_graph_1(its):
            sums = {}
            for it in its:
                o_acc = bank(OUT_BANK_1[it], [P, H])
                multiply_second(o_acc[:], 1, it, slice(0, H))
                biased = outp.tile([P, H], F32, name="biased")
                nc.vector.tensor_tensor(out=biased[:], in0=o_acc[:], in1=bias_all[:], op=ALU.add)
                sums[it] = biased
            return sums

        def relu_and_store(b, sums):
            for it, biased in sums.items():
                result = outp.tile([P, H], F32, name="result")
                nc.scalar.activation(out=result[:], in_=biased[:], func=ACT.Relu)
                nc.sync.dma_start(out=out[b, it * P : (it + 1) * P, :], in_=result[:])

        z_last = {}
        z_grouped = {}
        o_last = {}

        def z_of_part(i, xs, halves):
            part = LAST_PARTS[i]
            if 0 in halves:
                z_last[i] = bank(LAST_BANK[i], [P, part[1] - part[0]])
            for half in halves:
                for step in range(PASSES // 2):
                    g = half * PASSES // 2 + step
                    multiply(z_last[i][:], xs[half], step, g, slice(*part), g == 0, g == PASSES - 1)

        def regroup_part(i):
            cols = slice(*LAST_PARTS[i])
            nc.scalar.copy(out=z_flat[0][:, TILES - 1, cols], in_=z_last[i][:])
            z_grouped[i] = regroup(z_flat[0][:, :, cols], LAST_SHARE[i])

        def quantise_part(i):
            cols = slice(*LAST_PARTS[i])
            quantise(z_grouped[i], z_codes[0][:, cols], z_scales[0][:, cols])

        def second_of_part(i):
            part = LAST_PARTS[i]
            per = H // (part[1] - part[0])
            o_last[i] = []
            for n, first in enumerate(range(0, TILES, per)):
                o_acc = bank(OUT_BANK_0[i][n], [P, per, part[1] - part[0]])
                for it in range(per):
                    multiply_second(o_acc[:, it, :], 0, first + it, slice(*part))
                o_last[i].append(o_acc)

        def finish_part(i, n, first, count):
            part = LAST_PARTS[i]
            cols = slice(*part)
            width = part[1] - part[0]
            row = n * (H // width) + first
            biased = outp.tile([P, H], F32, name="biased")[:, : count * width].rearrange("p (i c) -> p i c", i=count)
            nc.vector.tensor_tensor(
                out=biased, in0=o_last[i][n][:, first : first + count, :],
                in1=bias_all[:, cols].unsqueeze(1).to_broadcast([P, count, width]), op=ALU.add,
            )
            result = outp.tile([P, H], F32, name="result")[:, : count * width].rearrange("p (i c) -> p i c", i=count)
            nc.scalar.activation(out=result, in_=biased, func=ACT.Relu)
            nc.sync.dma_start(
                out=out[0, row * P : (row + count) * P, cols].rearrange("(i p) c -> p i c", i=count),
                in_=result,
            )

        ready = prepare_round(0, lambda: None)
        bias_sum = bank(4, [P, H])
        nc.tensor.matmul(out=bias_sum[:], lhsT=ones[:], rhs=bias_rows[:], start=True, stop=True)
        nc.scalar.copy(out=bias_all[:], in_=bias_sum[:])
        sums = {}
        for j in range(LAST + 1):
            n = len(ROUNDS[j])
            if j < HALF:
                steps = [(blk, g2) for g2 in range(2) for blk in range(n)]
            else:
                steps = [(blk, g2) for blk in range(n) for g2 in range(2)]
            early = n if j < HALF else 0
            following = None
            if j < LAST:
                following = prepare_round(j + 1, lambda: multiply_round(j, ready, steps[:early]))
            relu_and_store(1, sums)
            sums = {}
            if j < LAST - 1:
                multiply_round(j, ready, steps[early:])
            elif j == LAST - 1:
                x_last = [ready, following]
                z_of_part(0, x_last, [0])
                z_of_part(1, x_last, [0])
                z_of_part(2, x_last, [0])
            else:
                z_of_part(0, x_last, [1])
                z_of_part(1, x_last, [1])
                z_of_part(2, x_last, [1])
                regroup_part(0)
                regroup_part(1)
                quantise_part(0)
                second_of_part(0)
                quantise_part(1)
                second_of_part(1)
                regroup_part(2)
                finish_part(0, 0, 0, 2)
                quantise_part(2)
                second_of_part(2)
                finish_part(0, 1, 0, 2)
                finish_part(1, 0, 0, 4)
                finish_part(2, 0, 0, 2)
                finish_part(2, 0, 2, 2)
            ready = following
            if j == C_AT - 1:
                add_rows_of_adj(1)
                add_rows_of_adj(0)
            for b in range(B):
                if j == C_AT + 1 + (1 - b):
                    d_columns(b, j)
            for b in range(B):
                if j == C_AT + (1 - b):
                    column_sums(b, j)
            for b, step in A_AT.get(j, []):
                if step < TILES:
                    products_of_d(b, step)
                elif step == TILES:
                    mask_a(b)
                else:
                    quantise_a(b)
            if j == HALF + 2 + HALF:
                quantise(regroup(z_flat[1][:], Z1_SHARE), z_codes[1][:], z_scales[1][:])
            if j in SECOND_AFTER:
                sums = second_of_graph_1(SECOND_AFTER[j])
